import numpy as np
import ml_dtypes


def mxq(x, axis, fmt="e4m3"):
    dtype, down = {"e4m3": (ml_dtypes.float8_e4m3fn, 7), "e5m2": (ml_dtypes.float8_e5m2, 14)}[fmt]
    v = np.moveaxis(np.asarray(x, np.float32).astype(ml_dtypes.bfloat16).astype(np.float64), axis, -1)
    blocks = v.reshape(v.shape[:-1] + (-1, 32))
    amax = np.abs(blocks).max(-1, keepdims=True)
    byte = np.maximum(np.where(amax > 0, np.frexp(amax)[1] - 1 + 127, 0) - down, 1)
    scale = np.exp2(byte - 127.0)
    codes = (blocks / scale).astype(np.float32).astype(dtype).astype(np.float64)
    return np.moveaxis((codes * scale).reshape(v.shape), -1, axis)


WIDE = False


def mx_kscale(k):
    if not WIDE:
        return np.ones(k)
    levels = np.array([10, -10, 5, -5, 0])
    a = np.random.permutation(np.resize(levels, k // 512 * 4)).reshape(k // 512, 4)
    idx = np.arange(k)
    return np.exp2(a[idx // 512, idx % 128 // 32])


BF16 = ml_dtypes.bfloat16


def bf(x):
    return np.asarray(x, np.float32).astype(BF16)


def f64(x):
    return np.asarray(x).astype(np.float64)


E2M1 = np.array([0.0, 0.5, 1.0, 1.5, 2.0, 3.0, 4.0, 6.0, -0.0, -0.5, -1.0, -1.5, -2.0, -3.0, -4.0, -6.0])


def pack_weight(w, fmt):
    k, n = w.shape
    w = f64(bf(w)).reshape(k // 32, 32, n)
    amax = np.abs(w).max(1)
    if fmt == "e4m3":
        byte = np.frexp(amax)[1] - 1 + 127 - 7
    else:
        mant, ex = np.frexp(amax / 6.0)
        byte = np.where(mant > 0.5, ex, ex - 1) + 127
    byte = np.clip(np.where(amax > 0, byte, 1), 1, 254)
    scaled = (w * np.exp2(127.0 - byte)[:, None, :]).reshape(k, n).astype(np.float32)
    by_word = np.ascontiguousarray(scaled.reshape(k // 512, 128, 4, n).transpose(0, 1, 3, 2))
    if fmt == "e4m3":
        words = by_word.astype(ml_dtypes.float8_e4m3fn).view(np.uint8)
    else:
        c = by_word.astype(ml_dtypes.float4_e2m1fn).view(np.uint8) & 0xF
        words = c[..., 0::2] | (c[..., 1::2] << 4)
    return np.ascontiguousarray(words), np.ascontiguousarray(byte.astype(np.uint8).reshape(k // 512, 16, n))


def unpack_weight(words, scales, fmt):
    g, p, n, _ = words.shape
    if fmt == "e4m3":
        vals = np.ascontiguousarray(words).view(ml_dtypes.float8_e4m3fn).astype(np.float64)
    else:
        nib = np.empty((g, p, n, 4), np.uint8)
        nib[..., 0::2] = words & 0xF
        nib[..., 1::2] = words >> 4
        vals = E2M1[nib]
    vals = vals * np.repeat(np.exp2(scales.astype(np.float64) - 127.0), 8, axis=1)[..., None]
    return vals.transpose(0, 1, 3, 2).reshape(g * 512, n)


B, S, I, O, NB, G = 2, 128, 16384, 128, 5, 1


def setup_inputs():
    s = mx_kscale(I)
    x = bf(np.random.standard_normal((B, S, I)) * s)
    basis_coeffs = bf(np.random.standard_normal((I, O // G, NB)) / np.sqrt(I))
    linear_w = np.random.standard_normal((O, I)) / np.sqrt(I) / s
    linear_w_words, linear_w_scales = pack_weight(np.ascontiguousarray(linear_w.T), "e4m3")
    pathway_balance = bf(0.5 + 0.1 * np.random.standard_normal(2))
    return {"x": x,
            "basis_coeffs": basis_coeffs,
            "linear_w_words": linear_w_words,
            "linear_w_scales": linear_w_scales,
            "pathway_balance": pathway_balance}


def reference(x, basis_coeffs, linear_w_words, linear_w_scales, pathway_balance):
    x = f64(x)
    pathway_balance = f64(pathway_balance)
    shape = x.shape[:-1]
    x_flat = x.reshape(-1, I)
    x_norm = np.tanh(x_flat)
    powers = np.arange(NB, dtype=np.float64)
    basis = x_norm[..., None] ** powers
    bq = mxq(basis, 1, "e4m3").transpose(2, 0, 1)
    cq = mxq(f64(basis_coeffs), 0, "e4m3").transpose(2, 0, 1)
    nonlinear_out = (bq @ cq).sum(0)
    if G > 1:
        nonlinear_out = np.tile(nonlinear_out, (1, G))
    linear_out = mxq(x_flat, 1, "e4m3") @ unpack_weight(linear_w_words, linear_w_scales, "e4m3")
    y = pathway_balance[0] * nonlinear_out + pathway_balance[1] * linear_out
    return y.reshape(*shape, O)

@@ -1,0 +1,270 @@
+from contextlib import ExitStack
+
+import concourse.mybir as mybir
+from concourse.masks import make_identity
+
+F32 = mybir.dt.float32
+BF16 = mybir.dt.bfloat16
+U32 = mybir.dt.uint32
+U8 = mybir.dt.uint8
+I32 = mybir.dt.int32
+FP8X4 = mybir.dt.float8_e4m3fn_x4
+ACT = mybir.ActivationFunctionType
+ALU = mybir.AluOpType
+
+P = 128
+PACK = 4
+K_PASS = P * PACK
+HALVES = 2
+ROWS = HALVES * P
+FEATURES = 16384
+OUTPUTS = 128
+POWERS = 5
+GROUPS = FEATURES // K_PASS
+G_CHUNK = 2
+K_CHUNK = G_CHUNK * K_PASS
+CHUNKS = GROUPS // G_CHUNK
+ACT_COLS = G_CHUNK * ROWS * PACK
+COEF_COLS = G_CHUNK * POWERS * OUTPUTS * PACK
+WIDEST_QUANTISE = 4096
+
+FLOPS = 2 * ROWS * FEATURES * OUTPUTS * (POWERS + 1)
+
+
+def tile_kolmogorovarnoldlinear_k_kernel(
+    tc, x, basis_coeffs, linear_w_words, linear_w_scales, pathway_balance, out
+):
+    nc = tc.nc
+
+    x_by_chunk = x.rearrange("h r (c k) -> c r h k", k=K_CHUNK)
+    coef_by_chunk = basis_coeffs.rearrange(
+        "(c g p j) o n -> c p g (j o n)", g=G_CHUNK, p=P, j=PACK
+    )
+
+    with ExitStack() as ctx:
+        const = ctx.enter_context(tc.tile_pool(name="const", bufs=1))
+        loads = ctx.enter_context(tc.tile_pool(name="loads", bufs=3))
+        work = ctx.enter_context(tc.tile_pool(name="work", bufs=2))
+        act_mx = ctx.enter_context(tc.tile_pool(name="act_mx", bufs=2))
+        coef_mx = ctx.enter_context(tc.tile_pool(name="coef_mx", bufs=3))
+        sums = ctx.enter_context(tc.psum_pool(name="sums", bufs=1))
+        turned = ctx.enter_context(tc.psum_pool(name="turned", bufs=2 * G_CHUNK))
+        ctx.enter_context(tc.manual_schedule())
+
+
+        def load_x(c):
+            x_rows = loads.tile([P, HALVES, K_CHUNK], BF16)
+            nc.sync.dma_start(out=x_rows[:], in_=x_by_chunk[c])
+            return x_rows
+
+        def load_coef(c):
+            coef_rows = loads.tile([P, G_CHUNK, PACK * OUTPUTS * POWERS], BF16)
+            nc.sync.dma_start(out=coef_rows[:], in_=coef_by_chunk[c])
+            return coef_rows
+
+        def turn_x(x_rows):
+            x_words = x_rows[:].bitcast(F32)
+            banks = []
+            for g in range(G_CHUNK):
+                bank = turned.tile([P, 2, ROWS], F32)
+                for u in range(2):
+                    for h in range(HALVES):
+                        nc.tensor.transpose(
+                            bank[:, u, h * P : (h + 1) * P],
+                            x_words[:, h, g * 2 * P + u : (g + 1) * 2 * P : 2],
+                            identity[:],
+                        )
+                banks.append(bank)
+            return banks
+
+        def new_activations():
+            x_grouped = work.tile([P, G_CHUNK, ROWS * PACK], BF16, align_bytes=64)
+            t_f32 = work.tile([P, G_CHUNK, ROWS * PACK], F32)
+            t_grouped = work.tile([P, G_CHUNK, ROWS * PACK], BF16, align_bytes=64)
+            return {"x": x_grouped, "t_f32": t_f32, "t": t_grouped}
+
+        def leave_psum(tiles, banks, g):
+            bank = banks[g]
+            nc.scalar.copy(
+                out=tiles["x"][:, g, :].bitcast(F32).rearrange("p (r u) -> p r u", u=2),
+                in_=bank[:].rearrange("p u r -> p r u"),
+            )
+            x_values = bank[:].bitcast(BF16).rearrange("p u (r e) -> p r u e", e=2)
+            nc.scalar.activation(
+                out=tiles["t_f32"][:, g, :].rearrange("p (r u e) -> p r u e", u=2, e=2),
+                in_=x_values,
+                func=ACT.Tanh,
+            )
+            nc.scalar.activation(
+                out=tiles["t"][:, g, :].rearrange("p (r u e) -> p r u e", u=2, e=2),
+                in_=x_values,
+                func=ACT.Tanh,
+            )
+
+        def flat(tile):
+            return tile[:].rearrange("p g f -> p (g f)")
+
+        def quantise(values, name):
+            words = act_mx.tile([P, ACT_COLS // PACK], U32, name=name + "_words", align_bytes=64)
+            scales = act_mx.tile([P, ACT_COLS // PACK], U8, name=name + "_scales", align_bytes=64)
+            nc.vector.quantize_mx(out=words[:].bitcast(FP8X4), scales=scales[:], in_=flat(values))
+            return words, scales
+
+        def regroup_coef(coef_rows):
+            coef_grouped = work.tile([P, G_CHUNK, POWERS, OUTPUTS, PACK], BF16, align_bytes=64)
+            nc.vector.tensor_copy(
+                out=coef_grouped[:],
+                in_=coef_rows[:].rearrange("p g (j o n) -> p g n o j", j=PACK, o=OUTPUTS, n=POWERS),
+            )
+            return coef_grouped
+
+        def quantise_coef(coef_grouped):
+            coef_words = coef_mx.tile([P, COEF_COLS // PACK], U32, align_bytes=64)
+            coef_scales = coef_mx.tile([P, COEF_COLS // PACK], U8, align_bytes=64)
+            values = coef_grouped[:].rearrange("p g n o j -> p (g n o j)")
+            for first in range(0, COEF_COLS, WIDEST_QUANTISE):
+                last = min(first + WIDEST_QUANTISE, COEF_COLS)
+                nc.vector.quantize_mx(
+                    out=coef_words[:, first // PACK : last // PACK].bitcast(FP8X4),
+                    scales=coef_scales[:, first // PACK : last // PACK],
+                    in_=values[:, first:last],
+                )
+            return coef_words, coef_scales
+
+        def multiply(c, operands, coef):
+            coef_words, coef_scales = coef
+            for name, n in (("x", None), ("ones", 0), ("t", 1), ("t4", 4), ("t2", 2), ("t3", 3)):
+                words, scales = operands[name]
+                for g in range(G_CHUNK):
+                    group = c * G_CHUNK + g
+                    for h in range(HALVES):
+                        rows = slice(0, P) if name == "ones" else slice((g * HALVES + h) * P, (g * HALVES + h + 1) * P)
+                        if name == "x":
+                            weights = w_words[:, group, :]
+                            weight_scales = w_scales[:, group, :]
+                            total = linear_sum[h]
+                        else:
+                            outputs = slice((g * POWERS + n) * OUTPUTS, (g * POWERS + n + 1) * OUTPUTS)
+                            weights = coef_words[:, outputs]
+                            weight_scales = coef_scales[:, outputs]
+                            total = basis_sum[h]
+                        nc.tensor.matmul_mx(
+                            out=total[:],
+                            lhsT=words[:, rows].bitcast(FP8X4),
+                            lhsT_scale=scales[:, rows],
+                            rhs=weights.bitcast(FP8X4),
+                            rhs_scale=weight_scales,
+                            start=(group == 0 and name in ("x", "ones")),
+                            stop=(group == GROUPS - 1 and name in ("x", "t3")),
+                        )
+
+
+        warm = const.tile([P, 1], F32)
+        nc.vector.memset(warm[:], 0.0)
+        nc.scalar.activation(out=warm[:], in_=warm[:], func=ACT.Tanh)
+
+        identity = const.tile([P, P], F32)
+        make_identity(nc, identity[:])
+
+        ones = const.tile([P, P * PACK], BF16, align_bytes=64)
+        nc.vector.memset(ones[:], 1.0)
+        ones_words = const.tile([P, P], U32, align_bytes=64)
+        ones_scales = const.tile([P, P], U8, align_bytes=64)
+        nc.vector.quantize_mx(out=ones_words[:].bitcast(FP8X4), scales=ones_scales[:], in_=ones[:])
+
+        w_scales = const.tile([P, GROUPS, OUTPUTS], U8, align_bytes=64)
+        nc.vector.memset(w_scales[:].rearrange("p g o -> p (g o)").bitcast(I32), 0)
+        w_words = const.tile([P, GROUPS, OUTPUTS], U32, align_bytes=64)
+        balance_bf16 = const.tile([P, 2], BF16)
+        balance = const.tile([P, 2], F32)
+
+        basis_sum = [sums.tile([P, OUTPUTS], F32, name="basis_sum%d" % h) for h in range(HALVES)]
+        linear_sum = [sums.tile([P, OUTPUTS], F32, name="linear_sum%d" % h) for h in range(HALVES)]
+
+
+        x_rows = {}
+        coef_rows = {}
+        x_rows[0] = load_x(0)
+        coef_rows[0] = load_coef(0)
+        coef_rows[1] = load_coef(1)
+        x_rows[1] = load_x(1)
+        nc.sync.dma_start(out=balance_bf16[:], in_=pathway_balance.partition_broadcast(P))
+        for quadrant in range(4):
+            nc.sync.dma_start(
+                out=w_scales[32 * quadrant : 32 * quadrant + 4, :, :].bitcast(I32),
+                in_=linear_w_scales[:, 4 * quadrant : 4 * quadrant + 4, :]
+                .rearrange("g q o -> q g o")
+                .bitcast(I32),
+            )
+        nc.sync.dma_start(
+            out=w_words[:].bitcast(I32),
+            in_=linear_w_words.rearrange("g p o j -> p g (o j)").bitcast(I32),
+        )
+        coef_rows[2] = load_coef(2)
+        x_rows[2] = load_x(2)
+
+        banks = {0: turn_x(x_rows[0]), 1: turn_x(x_rows[1])}
+
+        grouped = {0: regroup_coef(coef_rows[0]), 1: regroup_coef(coef_rows[1])}
+        coef = {0: quantise_coef(grouped[0]), 1: quantise_coef(grouped[1])}
+        nc.vector.tensor_copy(out=balance[:], in_=balance_bf16[:])
+
+        tiles = {0: new_activations()}
+        for g in range(G_CHUNK):
+            leave_psum(tiles[0], banks[0], g)
+
+
+        for c in range(CHUNKS):
+            if c + 3 < CHUNKS:
+                x_rows[c + 3] = load_x(c + 3)
+                coef_rows[c + 3] = load_coef(c + 3)
+            if c + 2 < CHUNKS:
+                banks[c + 2] = turn_x(x_rows[c + 2])
+
+            now = tiles[c]
+            t2_f32 = work.tile([P, G_CHUNK, ROWS * PACK], F32)
+            t4_grouped = work.tile([P, G_CHUNK, ROWS * PACK], BF16, align_bytes=64)
+            nc.scalar.activation(out=flat(t2_f32), in_=flat(now["t_f32"]), func=ACT.Square)
+            if c + 1 < CHUNKS:
+                tiles[c + 1] = new_activations()
+                leave_psum(tiles[c + 1], banks[c + 1], 0)
+            nc.scalar.activation(out=flat(t4_grouped), in_=flat(t2_f32), func=ACT.Square)
+            if c + 1 < CHUNKS:
+                leave_psum(tiles[c + 1], banks[c + 1], 1)
+
+            if c + 2 < CHUNKS:
+                grouped[c + 2] = regroup_coef(coef_rows[c + 2])
+            operands = {"ones": (ones_words, ones_scales)}
+            operands["x"] = quantise(now["x"], "x")
+            operands["t"] = quantise(now["t"], "t")
+            t2_grouped = work.tile([P, G_CHUNK, ROWS * PACK], BF16, align_bytes=64)
+            t3_grouped = work.tile([P, G_CHUNK, ROWS * PACK], BF16, align_bytes=64)
+            nc.vector.tensor_copy(out=flat(t2_grouped), in_=flat(t2_f32))
+            nc.vector.tensor_tensor(
+                out=flat(t3_grouped), in0=flat(t2_f32), in1=flat(now["t_f32"]), op=ALU.mult
+            )
+            if c + 2 < CHUNKS:
+                coef[c + 2] = quantise_coef(grouped[c + 2])
+            operands["t4"] = quantise(t4_grouped, "t4")
+            operands["t2"] = quantise(t2_grouped, "t2")
+            operands["t3"] = quantise(t3_grouped, "t3")
+
+            multiply(c, operands, coef[c])
+
+
+        linear_part = const.tile([P, HALVES, OUTPUTS], F32)
+        y = const.tile([P, HALVES, OUTPUTS], F32)
+        for h in range(HALVES):
+            nc.scalar.activation(
+                out=linear_part[:, h, :], in_=linear_sum[h][:], func=ACT.Copy, scale=balance[:, 1:2]
+            )
+        for h in range(HALVES):
+            nc.vector.scalar_tensor_tensor(
+                out=y[:, h, :],
+                in0=basis_sum[h][:],
+                scalar=balance[:, 0:1],
+                in1=linear_part[:, h, :],
+                op0=ALU.mult,
+                op1=ALU.add,
+            )
+            nc.sync.dma_start(out=out[h], in_=y[:, h, :])

@@ -112,9 +112,16 @@ def tile_kolmogorovarnoldlinear_k_kernel(
 
         def regroup_coef(coef_rows):
             coef_grouped = work.tile([P, G_CHUNK, POWERS, OUTPUTS, PACK], BF16, align_bytes=64)
+            by_output_in = coef_rows[:].rearrange(
+                "p g (j o n) -> p g o n j", j=PACK, o=OUTPUTS, n=POWERS
+            )
+            by_output_out = coef_grouped[:].rearrange("p g n o j -> p g o n j")
+            together = POWERS - 1
             nc.vector.tensor_copy(
-                out=coef_grouped[:],
-                in_=coef_rows[:].rearrange("p g (j o n) -> p g n o j", j=PACK, o=OUTPUTS, n=POWERS),
+                out=by_output_out[:, :, :, 0:together, :], in_=by_output_in[:, :, :, 0:together, :]
+            )
+            nc.vector.tensor_copy(
+                out=by_output_out[:, :, :, together, :], in_=by_output_in[:, :, :, together, :]
             )
             return coef_grouped
 

@@ -120,7 +120,7 @@ def tile_kolmogorovarnoldlinear_k_kernel(
             nc.vector.tensor_copy(
                 out=by_output_out[:, :, :, 0:together, :], in_=by_output_in[:, :, :, 0:together, :]
             )
-            nc.vector.tensor_copy(
+            nc.scalar.copy(
                 out=by_output_out[:, :, :, together, :], in_=by_output_in[:, :, :, together, :]
             )
             return coef_grouped
@@ -228,6 +228,9 @@ def tile_kolmogorovarnoldlinear_k_kernel(
             if c + 2 < CHUNKS:
                 banks[c + 2] = turn_x(x_rows[c + 2])
 
+            if c + 2 < CHUNKS:
+                grouped[c + 2] = regroup_coef(coef_rows[c + 2])
+
             now = tiles[c]
             t2_f32 = work.tile([P, G_CHUNK, ROWS * PACK], F32)
             t4_grouped = work.tile([P, G_CHUNK, ROWS * PACK], BF16, align_bytes=64)
@@ -239,8 +242,6 @@ def tile_kolmogorovarnoldlinear_k_kernel(
             if c + 1 < CHUNKS:
                 leave_psum(tiles[c + 1], banks[c + 1], 1)
 
-            if c + 2 < CHUNKS:
-                grouped[c + 2] = regroup_coef(coef_rows[c + 2])
             operands = {"ones": (ones_words, ones_scales)}
             operands["x"] = quantise(now["x"], "x")
             operands["t"] = quantise(now["t"], "t")

@@ -27,6 +27,7 @@ CHUNKS = GROUPS // G_CHUNK
 ACT_COLS = G_CHUNK * ROWS * PACK
 COEF_COLS = G_CHUNK * POWERS * OUTPUTS * PACK
 WIDEST_QUANTISE = 4096
+SCALAR_OUTPUTS = 64
 
 FLOPS = 2 * ROWS * FEATURES * OUTPUTS * (POWERS + 1)
 
@@ -78,15 +79,14 @@ def tile_kolmogorovarnoldlinear_k_kernel(
             return banks
 
         def new_activations():
-            x_grouped = work.tile([P, G_CHUNK, ROWS * PACK], BF16, align_bytes=64)
+            x_and_t = work.tile([P, 2, G_CHUNK, ROWS * PACK], BF16, align_bytes=64)
             t_f32 = work.tile([P, G_CHUNK, ROWS * PACK], F32)
-            t_grouped = work.tile([P, G_CHUNK, ROWS * PACK], BF16, align_bytes=64)
-            return {"x": x_grouped, "t_f32": t_f32, "t": t_grouped}
+            return {"x_and_t": x_and_t, "t_f32": t_f32}
 
         def leave_psum(tiles, banks, g):
             bank = banks[g]
             nc.scalar.copy(
-                out=tiles["x"][:, g, :].bitcast(F32).rearrange("p (r u) -> p r u", u=2),
+                out=tiles["x_and_t"][:, 0, g, :].bitcast(F32).rearrange("p (r u) -> p r u", u=2),
                 in_=bank[:].rearrange("p u r -> p r u"),
             )
             x_values = bank[:].bitcast(BF16).rearrange("p u (r e) -> p r u e", e=2)
@@ -96,7 +96,7 @@ def tile_kolmogorovarnoldlinear_k_kernel(
                 func=ACT.Tanh,
             )
             nc.scalar.activation(
-                out=tiles["t"][:, g, :].rearrange("p (r u e) -> p r u e", u=2, e=2),
+                out=tiles["x_and_t"][:, 1, g, :].rearrange("p (r u e) -> p r u e", u=2, e=2),
                 in_=x_values,
                 func=ACT.Tanh,
             )
@@ -104,11 +104,12 @@ def tile_kolmogorovarnoldlinear_k_kernel(
         def flat(tile):
             return tile[:].rearrange("p g f -> p (g f)")
 
-        def quantise(values, name):
-            words = act_mx.tile([P, ACT_COLS // PACK], U32, name=name + "_words", align_bytes=64)
-            scales = act_mx.tile([P, ACT_COLS // PACK], U8, name=name + "_scales", align_bytes=64)
-            nc.vector.quantize_mx(out=words[:].bitcast(FP8X4), scales=scales[:], in_=flat(values))
-            return words, scales
+        def quantise(values, names):
+            columns = len(names) * ACT_COLS // PACK
+            words = act_mx.tile([P, columns], U32, name=names[0] + "_words", align_bytes=64)
+            scales = act_mx.tile([P, columns], U8, name=names[0] + "_scales", align_bytes=64)
+            nc.vector.quantize_mx(out=words[:].bitcast(FP8X4), scales=scales[:], in_=values)
+            return [(words, scales, i * ACT_COLS // PACK) for i in range(len(names))]
 
         def regroup_coef(coef_rows):
             coef_grouped = work.tile([P, G_CHUNK, POWERS, OUTPUTS, PACK], BF16, align_bytes=64)
@@ -120,10 +121,20 @@ def tile_kolmogorovarnoldlinear_k_kernel(
             nc.vector.tensor_copy(
                 out=by_output_out[:, :, :, 0:together, :], in_=by_output_in[:, :, :, 0:together, :]
             )
-            nc.scalar.copy(
-                out=by_output_out[:, :, :, together, :], in_=by_output_in[:, :, :, together, :]
+            mine = OUTPUTS - SCALAR_OUTPUTS
+            nc.vector.tensor_copy(
+                out=by_output_out[:, :, 0:mine, together, :], in_=by_output_in[:, :, 0:mine, together, :]
             )
             return coef_grouped
+
+        def regroup_rest(coef_rows, coef_grouped):
+            first = OUTPUTS - SCALAR_OUTPUTS
+            nc.scalar.copy(
+                out=coef_grouped[:, :, POWERS - 1, first:OUTPUTS, :],
+                in_=coef_rows[:].rearrange("p g (j o n) -> p g n o j", j=PACK, o=OUTPUTS, n=POWERS)[
+                    :, :, POWERS - 1, first:OUTPUTS, :
+                ],
+            )
 
         def quantise_coef(coef_grouped):
             coef_words = coef_mx.tile([P, COEF_COLS // PACK], U32, align_bytes=64)
@@ -141,11 +152,12 @@ def tile_kolmogorovarnoldlinear_k_kernel(
         def multiply(c, operands, coef):
             coef_words, coef_scales = coef
             for name, n in (("x", None), ("ones", 0), ("t", 1), ("t4", 4), ("t2", 2), ("t3", 3)):
-                words, scales = operands[name]
+                words, scales, first_column = operands[name]
                 for g in range(G_CHUNK):
                     group = c * G_CHUNK + g
                     for h in range(HALVES):
-                        rows = slice(0, P) if name == "ones" else slice((g * HALVES + h) * P, (g * HALVES + h + 1) * P)
+                        first_row = first_column if name == "ones" else first_column + (g * HALVES + h) * P
+                        rows = slice(first_row, first_row + P)
                         if name == "x":
                             weights = w_words[:, group, :]
                             weight_scales = w_scales[:, group, :]
@@ -213,12 +225,13 @@ def tile_kolmogorovarnoldlinear_k_kernel(
         banks = {0: turn_x(x_rows[0]), 1: turn_x(x_rows[1])}
 
         grouped = {0: regroup_coef(coef_rows[0]), 1: regroup_coef(coef_rows[1])}
-        coef = {0: quantise_coef(grouped[0]), 1: quantise_coef(grouped[1])}
-        nc.vector.tensor_copy(out=balance[:], in_=balance_bf16[:])
-
         tiles = {0: new_activations()}
         for g in range(G_CHUNK):
             leave_psum(tiles[0], banks[0], g)
+        regroup_rest(coef_rows[0], grouped[0])
+        regroup_rest(coef_rows[1], grouped[1])
+        coef = {0: quantise_coef(grouped[0]), 1: quantise_coef(grouped[1])}
+        nc.vector.tensor_copy(out=balance[:], in_=balance_bf16[:])
 
 
         for c in range(CHUNKS):
@@ -235,6 +248,8 @@ def tile_kolmogorovarnoldlinear_k_kernel(
             t2_f32 = work.tile([P, G_CHUNK, ROWS * PACK], F32)
             t4_grouped = work.tile([P, G_CHUNK, ROWS * PACK], BF16, align_bytes=64)
             nc.scalar.activation(out=flat(t2_f32), in_=flat(now["t_f32"]), func=ACT.Square)
+            if c + 2 < CHUNKS:
+                regroup_rest(coef_rows[c + 2], grouped[c + 2])
             if c + 1 < CHUNKS:
                 tiles[c + 1] = new_activations()
                 leave_psum(tiles[c + 1], banks[c + 1], 0)
@@ -242,20 +257,26 @@ def tile_kolmogorovarnoldlinear_k_kernel(
             if c + 1 < CHUNKS:
                 leave_psum(tiles[c + 1], banks[c + 1], 1)
 
-            operands = {"ones": (ones_words, ones_scales)}
-            operands["x"] = quantise(now["x"], "x")
-            operands["t"] = quantise(now["t"], "t")
-            t2_grouped = work.tile([P, G_CHUNK, ROWS * PACK], BF16, align_bytes=64)
-            t3_grouped = work.tile([P, G_CHUNK, ROWS * PACK], BF16, align_bytes=64)
-            nc.vector.tensor_copy(out=flat(t2_grouped), in_=flat(t2_f32))
+            operands = {"ones": (ones_words, ones_scales, 0)}
+            operands["x"], operands["t"] = quantise(
+                now["x_and_t"][:].rearrange("p a g f -> p (a g f)"), ("x", "t")
+            )
+            t2_and_t3 = work.tile([P, 2, G_CHUNK, ROWS * PACK], BF16, align_bytes=64)
+            nc.vector.tensor_copy(
+                out=t2_and_t3[:, 0, :, :].rearrange("p g f -> p (g f)"), in_=flat(t2_f32)
+            )
             nc.vector.tensor_tensor(
-                out=flat(t3_grouped), in0=flat(t2_f32), in1=flat(now["t_f32"]), op=ALU.mult
+                out=t2_and_t3[:, 1, :, :].rearrange("p g f -> p (g f)"),
+                in0=flat(t2_f32),
+                in1=flat(now["t_f32"]),
+                op=ALU.mult,
             )
             if c + 2 < CHUNKS:
                 coef[c + 2] = quantise_coef(grouped[c + 2])
-            operands["t4"] = quantise(t4_grouped, "t4")
-            operands["t2"] = quantise(t2_grouped, "t2")
-            operands["t3"] = quantise(t3_grouped, "t3")
+            operands["t4"] = quantise(flat(t4_grouped), ("t4",))[0]
+            operands["t2"], operands["t3"] = quantise(
+                t2_and_t3[:].rearrange("p a g f -> p (a g f)"), ("t2", "t3")
+            )
 
             multiply(c, operands, coef[c])
 

@@ -207,6 +207,8 @@ def tile_kolmogorovarnoldlinear_k_kernel(
         coef_rows[0] = load_coef(0)
         coef_rows[1] = load_coef(1)
         x_rows[1] = load_x(1)
+        coef_rows[2] = load_coef(2)
+        x_rows[2] = load_x(2)
         nc.sync.dma_start(out=balance_bf16[:], in_=pathway_balance.partition_broadcast(P))
         for quadrant in range(4):
             nc.sync.dma_start(
@@ -219,8 +221,6 @@ def tile_kolmogorovarnoldlinear_k_kernel(
             out=w_words[:].bitcast(I32),
             in_=linear_w_words.rearrange("g p o j -> p g (o j)").bitcast(I32),
         )
-        coef_rows[2] = load_coef(2)
-        x_rows[2] = load_x(2)
 
         banks = {0: turn_x(x_rows[0]), 1: turn_x(x_rows[1])}
 

@@ -27,7 +27,7 @@ CHUNKS = GROUPS // G_CHUNK
 ACT_COLS = G_CHUNK * ROWS * PACK
 COEF_COLS = G_CHUNK * POWERS * OUTPUTS * PACK
 WIDEST_QUANTISE = 4096
-SCALAR_OUTPUTS = 64
+LAST = POWERS - 1
 
 FLOPS = 2 * ROWS * FEATURES * OUTPUTS * (POWERS + 1)
 
@@ -49,7 +49,8 @@ def tile_kolmogorovarnoldlinear_k_kernel(
         act_mx = ctx.enter_context(tc.tile_pool(name="act_mx", bufs=2))
         coef_mx = ctx.enter_context(tc.tile_pool(name="coef_mx", bufs=3))
         sums = ctx.enter_context(tc.psum_pool(name="sums", bufs=1))
-        turned = ctx.enter_context(tc.psum_pool(name="turned", bufs=2 * G_CHUNK))
+        turned = ctx.enter_context(tc.psum_pool(name="turned", bufs=3))
+        moved = ctx.enter_context(tc.psum_pool(name="moved", bufs=1))
         ctx.enter_context(tc.manual_schedule())
 
 
@@ -63,28 +64,24 @@ def tile_kolmogorovarnoldlinear_k_kernel(
             nc.sync.dma_start(out=coef_rows[:], in_=coef_by_chunk[c])
             return coef_rows
 
-        def turn_x(x_rows):
+        def turn_x(x_rows, g):
             x_words = x_rows[:].bitcast(F32)
-            banks = []
-            for g in range(G_CHUNK):
-                bank = turned.tile([P, 2, ROWS], F32)
-                for u in range(2):
-                    for h in range(HALVES):
-                        nc.tensor.transpose(
-                            bank[:, u, h * P : (h + 1) * P],
-                            x_words[:, h, g * 2 * P + u : (g + 1) * 2 * P : 2],
-                            identity[:],
-                        )
-                banks.append(bank)
-            return banks
+            bank = turned.tile([P, 2, ROWS], F32)
+            for u in range(2):
+                for h in range(HALVES):
+                    nc.tensor.transpose(
+                        bank[:, u, h * P : (h + 1) * P],
+                        x_words[:, h, g * 2 * P + u : (g + 1) * 2 * P : 2],
+                        identity[:],
+                    )
+            return bank
 
         def new_activations():
             x_and_t = work.tile([P, 2, G_CHUNK, ROWS * PACK], BF16, align_bytes=64)
             t_f32 = work.tile([P, G_CHUNK, ROWS * PACK], F32)
             return {"x_and_t": x_and_t, "t_f32": t_f32}
 
-        def leave_psum(tiles, banks, g):
-            bank = banks[g]
+        def leave_psum(tiles, bank, g):
             nc.scalar.copy(
                 out=tiles["x_and_t"][:, 0, g, :].bitcast(F32).rearrange("p (r u) -> p r u", u=2),
                 in_=bank[:].rearrange("p u r -> p r u"),
@@ -117,23 +114,28 @@ def tile_kolmogorovarnoldlinear_k_kernel(
                 "p g (j o n) -> p g o n j", j=PACK, o=OUTPUTS, n=POWERS
             )
             by_output_out = coef_grouped[:].rearrange("p g n o j -> p g o n j")
-            together = POWERS - 1
             nc.vector.tensor_copy(
-                out=by_output_out[:, :, :, 0:together, :], in_=by_output_in[:, :, :, 0:together, :]
-            )
-            mine = OUTPUTS - SCALAR_OUTPUTS
-            nc.vector.tensor_copy(
-                out=by_output_out[:, :, 0:mine, together, :], in_=by_output_in[:, :, 0:mine, together, :]
+                out=by_output_out[:, :, :, 0:LAST, :], in_=by_output_in[:, :, :, 0:LAST, :]
             )
             return coef_grouped
 
-        def regroup_rest(coef_rows, coef_grouped):
-            first = OUTPUTS - SCALAR_OUTPUTS
+        def move_last(coef_rows):
+            bank = moved.tile([P, G_CHUNK, OUTPUTS, PACK], BF16)
+            by_power = coef_rows[:].rearrange("p g (j o n) -> p g n o j", j=PACK, o=OUTPUTS, n=POWERS)
+            for g in range(G_CHUNK):
+                nc.tensor.matmul(
+                    out=bank[:, g, :, :],
+                    lhsT=identity_bf16[:],
+                    rhs=by_power[:, g, LAST, :, :],
+                    start=True,
+                    stop=True,
+                )
+            return bank
+
+        def regroup_last(bank, coef_grouped):
             nc.scalar.copy(
-                out=coef_grouped[:, :, POWERS - 1, first:OUTPUTS, :],
-                in_=coef_rows[:].rearrange("p g (j o n) -> p g n o j", j=PACK, o=OUTPUTS, n=POWERS)[
-                    :, :, POWERS - 1, first:OUTPUTS, :
-                ],
+                out=coef_grouped[:, :, LAST, :, :].rearrange("p g o j -> p g (o j)"),
+                in_=bank[:].rearrange("p g o j -> p g (o j)"),
             )
 
         def quantise_coef(coef_grouped):
@@ -184,6 +186,8 @@ def tile_kolmogorovarnoldlinear_k_kernel(
 
         identity = const.tile([P, P], F32)
         make_identity(nc, identity[:])
+        identity_bf16 = const.tile([P, P], BF16)
+        make_identity(nc, identity_bf16[:])
 
         ones = const.tile([P, P * PACK], BF16, align_bytes=64)
         nc.vector.memset(ones[:], 1.0)
@@ -222,14 +226,20 @@ def tile_kolmogorovarnoldlinear_k_kernel(
             in_=linear_w_words.rearrange("g p o j -> p g (o j)").bitcast(I32),
         )
 
-        banks = {0: turn_x(x_rows[0]), 1: turn_x(x_rows[1])}
+        banks = {}
+        for g in range(G_CHUNK):
+            banks[0, g] = turn_x(x_rows[0], g)
+        last = {0: move_last(coef_rows[0])}
 
         grouped = {0: regroup_coef(coef_rows[0]), 1: regroup_coef(coef_rows[1])}
         tiles = {0: new_activations()}
         for g in range(G_CHUNK):
-            leave_psum(tiles[0], banks[0], g)
-        regroup_rest(coef_rows[0], grouped[0])
-        regroup_rest(coef_rows[1], grouped[1])
+            leave_psum(tiles[0], banks[0, g], g)
+        regroup_last(last[0], grouped[0])
+        last[1] = move_last(coef_rows[1])
+        for g in range(G_CHUNK):
+            banks[1, g] = turn_x(x_rows[1], g)
+        regroup_last(last[1], grouped[1])
         coef = {0: quantise_coef(grouped[0]), 1: quantise_coef(grouped[1])}
         nc.vector.tensor_copy(out=balance[:], in_=balance_bf16[:])
 
@@ -239,7 +249,8 @@ def tile_kolmogorovarnoldlinear_k_kernel(
                 x_rows[c + 3] = load_x(c + 3)
                 coef_rows[c + 3] = load_coef(c + 3)
             if c + 2 < CHUNKS:
-                banks[c + 2] = turn_x(x_rows[c + 2])
+                last[c + 2] = move_last(coef_rows[c + 2])
+                banks[c + 2, 0] = turn_x(x_rows[c + 2], 0)
 
             if c + 2 < CHUNKS:
                 grouped[c + 2] = regroup_coef(coef_rows[c + 2])
@@ -249,13 +260,13 @@ def tile_kolmogorovarnoldlinear_k_kernel(
             t4_grouped = work.tile([P, G_CHUNK, ROWS * PACK], BF16, align_bytes=64)
             nc.scalar.activation(out=flat(t2_f32), in_=flat(now["t_f32"]), func=ACT.Square)
             if c + 2 < CHUNKS:
-                regroup_rest(coef_rows[c + 2], grouped[c + 2])
+                regroup_last(last[c + 2], grouped[c + 2])
             if c + 1 < CHUNKS:
                 tiles[c + 1] = new_activations()
-                leave_psum(tiles[c + 1], banks[c + 1], 0)
+                leave_psum(tiles[c + 1], banks[c + 1, 0], 0)
             nc.scalar.activation(out=flat(t4_grouped), in_=flat(t2_f32), func=ACT.Square)
             if c + 1 < CHUNKS:
-                leave_psum(tiles[c + 1], banks[c + 1], 1)
+                leave_psum(tiles[c + 1], banks[c + 1, 1], 1)
 
             operands = {"ones": (ones_words, ones_scales, 0)}
             operands["x"], operands["t"] = quantise(
@@ -279,6 +290,8 @@ def tile_kolmogorovarnoldlinear_k_kernel(
             )
 
             multiply(c, operands, coef[c])
+            if c + 2 < CHUNKS:
+                banks[c + 2, 1] = turn_x(x_rows[c + 2], 1)
 
 
         linear_part = const.tile([P, HALVES, OUTPUTS], F32)

@@ -44,7 +44,7 @@ def tile_kolmogorovarnoldlinear_k_kernel(
 
     with ExitStack() as ctx:
         const = ctx.enter_context(tc.tile_pool(name="const", bufs=1))
-        loads = ctx.enter_context(tc.tile_pool(name="loads", bufs=3))
+        loads = ctx.enter_context(tc.tile_pool(name="loads", bufs=4))
         work = ctx.enter_context(tc.tile_pool(name="work", bufs=2))
         act_mx = ctx.enter_context(tc.tile_pool(name="act_mx", bufs=2))
         coef_mx = ctx.enter_context(tc.tile_pool(name="coef_mx", bufs=3))
@@ -151,9 +151,9 @@ def tile_kolmogorovarnoldlinear_k_kernel(
                 )
             return coef_words, coef_scales
 
-        def multiply(c, operands, coef):
+        def multiply(c, operands, coef, factors):
             coef_words, coef_scales = coef
-            for name, n in (("x", None), ("ones", 0), ("t", 1), ("t4", 4), ("t2", 2), ("t3", 3)):
+            for name, n in factors:
                 words, scales, first_column = operands[name]
                 for g in range(G_CHUNK):
                     group = c * G_CHUNK + g
@@ -213,6 +213,8 @@ def tile_kolmogorovarnoldlinear_k_kernel(
         x_rows[1] = load_x(1)
         coef_rows[2] = load_coef(2)
         x_rows[2] = load_x(2)
+        coef_rows[3] = load_coef(3)
+        x_rows[3] = load_x(3)
         nc.sync.dma_start(out=balance_bf16[:], in_=pathway_balance.partition_broadcast(P))
         for quadrant in range(4):
             nc.sync.dma_start(
@@ -240,17 +242,15 @@ def tile_kolmogorovarnoldlinear_k_kernel(
         for g in range(G_CHUNK):
             banks[1, g] = turn_x(x_rows[1], g)
         regroup_last(last[1], grouped[1])
+        last[2] = move_last(coef_rows[2])
         coef = {0: quantise_coef(grouped[0]), 1: quantise_coef(grouped[1])}
         nc.vector.tensor_copy(out=balance[:], in_=balance_bf16[:])
 
 
         for c in range(CHUNKS):
-            if c + 3 < CHUNKS:
-                x_rows[c + 3] = load_x(c + 3)
-                coef_rows[c + 3] = load_coef(c + 3)
-            if c + 2 < CHUNKS:
-                last[c + 2] = move_last(coef_rows[c + 2])
-                banks[c + 2, 0] = turn_x(x_rows[c + 2], 0)
+            if c + 4 < CHUNKS:
+                x_rows[c + 4] = load_x(c + 4)
+                coef_rows[c + 4] = load_coef(c + 4)
 
             if c + 2 < CHUNKS:
                 grouped[c + 2] = regroup_coef(coef_rows[c + 2])
@@ -289,9 +289,13 @@ def tile_kolmogorovarnoldlinear_k_kernel(
                 t2_and_t3[:].rearrange("p a g f -> p (a g f)"), ("t2", "t3")
             )
 
-            multiply(c, operands, coef[c])
+            multiply(c, operands, coef[c], (("x", None), ("ones", 0), ("t", 1)))
+            if c + 3 < CHUNKS:
+                last[c + 3] = move_last(coef_rows[c + 3])
             if c + 2 < CHUNKS:
-                banks[c + 2, 1] = turn_x(x_rows[c + 2], 1)
+                for g in range(G_CHUNK):
+                    banks[c + 2, g] = turn_x(x_rows[c + 2], g)
+            multiply(c, operands, coef[c], (("t4", 4), ("t2", 2), ("t3", 3)))
 
 
         linear_part = const.tile([P, HALVES, OUTPUTS], F32)

@@ -25,9 +25,8 @@ G_CHUNK = 2
 K_CHUNK = G_CHUNK * K_PASS
 CHUNKS = GROUPS // G_CHUNK
 ACT_COLS = G_CHUNK * ROWS * PACK
-COEF_COLS = G_CHUNK * POWERS * OUTPUTS * PACK
-WIDEST_QUANTISE = 4096
 LAST = POWERS - 1
+LAST_COLUMN = G_CHUNK * LAST * OUTPUTS
 
 FLOPS = 2 * ROWS * FEATURES * OUTPUTS * (POWERS + 1)
 
@@ -37,7 +36,7 @@ def tile_kolmogorovarnoldlinear_k_kernel(
 ):
     nc = tc.nc
 
-    x_by_chunk = x.rearrange("h r (c k) -> c r h k", k=K_CHUNK)
+    x_by_group = x.rearrange("h r (g k) -> g r h k", k=K_PASS)
     coef_by_chunk = basis_coeffs.rearrange(
         "(c g p j) o n -> c p g (j o n)", g=G_CHUNK, p=P, j=PACK
     )
@@ -55,8 +54,9 @@ def tile_kolmogorovarnoldlinear_k_kernel(
 
 
         def load_x(c):
-            x_rows = loads.tile([P, HALVES, K_CHUNK], BF16)
-            nc.sync.dma_start(out=x_rows[:], in_=x_by_chunk[c])
+            x_rows = loads.tile([P, G_CHUNK, HALVES, K_PASS], BF16)
+            for g in range(G_CHUNK):
+                nc.sync.dma_start(out=x_rows[:, g, :, :], in_=x_by_group[c * G_CHUNK + g])
             return x_rows
 
         def load_coef(c):
@@ -64,14 +64,22 @@ def tile_kolmogorovarnoldlinear_k_kernel(
             nc.sync.dma_start(out=coef_rows[:], in_=coef_by_chunk[c])
             return coef_rows
 
+        def load_first_chunk():
+            x_rows = loads.tile([P, G_CHUNK, HALVES, K_PASS], BF16)
+            coef_rows = loads.tile([P, G_CHUNK, PACK * OUTPUTS * POWERS], BF16)
+            for g in range(G_CHUNK):
+                nc.sync.dma_start(out=x_rows[:, g, :, :], in_=x_by_group[g])
+                nc.sync.dma_start(out=coef_rows[:, g, :], in_=coef_by_chunk[0][:, g, :])
+            return x_rows, coef_rows
+
         def turn_x(x_rows, g):
-            x_words = x_rows[:].bitcast(F32)
+            x_words = x_rows[:, g, :, :].bitcast(F32)
             bank = turned.tile([P, 2, ROWS], F32)
             for u in range(2):
                 for h in range(HALVES):
                     nc.tensor.transpose(
                         bank[:, u, h * P : (h + 1) * P],
-                        x_words[:, h, g * 2 * P + u : (g + 1) * 2 * P : 2],
+                        x_words[:, h, u : 2 * P : 2],
                         identity[:],
                     )
             return bank
@@ -108,16 +116,19 @@ def tile_kolmogorovarnoldlinear_k_kernel(
             nc.vector.quantize_mx(out=words[:].bitcast(FP8X4), scales=scales[:], in_=values)
             return [(words, scales, i * ACT_COLS // PACK) for i in range(len(names))]
 
-        def regroup_coef(coef_rows):
-            coef_grouped = work.tile([P, G_CHUNK, POWERS, OUTPUTS, PACK], BF16, align_bytes=64)
+        def new_coef_grouped():
+            first_powers = work.tile([P, G_CHUNK, LAST, OUTPUTS, PACK], BF16, align_bytes=64)
+            last_power = work.tile([P, G_CHUNK, OUTPUTS, PACK], BF16, align_bytes=64)
+            return first_powers, last_power
+
+        def regroup_coef(coef_rows, first_powers, groups):
             by_output_in = coef_rows[:].rearrange(
                 "p g (j o n) -> p g o n j", j=PACK, o=OUTPUTS, n=POWERS
             )
-            by_output_out = coef_grouped[:].rearrange("p g n o j -> p g o n j")
+            by_output_out = first_powers[:].rearrange("p g n o j -> p g o n j")
             nc.vector.tensor_copy(
-                out=by_output_out[:, :, :, 0:LAST, :], in_=by_output_in[:, :, :, 0:LAST, :]
+                out=by_output_out[:, groups, :, :, :], in_=by_output_in[:, groups, :, 0:LAST, :]
             )
-            return coef_grouped
 
         def move_last(coef_rows):
             bank = moved.tile([P, G_CHUNK, OUTPUTS, PACK], BF16)
@@ -132,22 +143,23 @@ def tile_kolmogorovarnoldlinear_k_kernel(
                 )
             return bank
 
-        def regroup_last(bank, coef_grouped):
+        def regroup_last(bank, last_power):
             nc.scalar.copy(
-                out=coef_grouped[:, :, LAST, :, :].rearrange("p g o j -> p g (o j)"),
-                in_=bank[:].rearrange("p g o j -> p g (o j)"),
+                out=last_power[:].rearrange("p g o j -> p (g o j)"),
+                in_=bank[:].rearrange("p g o j -> p (g o j)"),
             )
 
-        def quantise_coef(coef_grouped):
-            coef_words = coef_mx.tile([P, COEF_COLS // PACK], U32, align_bytes=64)
-            coef_scales = coef_mx.tile([P, COEF_COLS // PACK], U8, align_bytes=64)
-            values = coef_grouped[:].rearrange("p g n o j -> p (g n o j)")
-            for first in range(0, COEF_COLS, WIDEST_QUANTISE):
-                last = min(first + WIDEST_QUANTISE, COEF_COLS)
+        def quantise_coef(first_powers, last_power):
+            coef_words = coef_mx.tile([P, G_CHUNK * POWERS * OUTPUTS], U32, align_bytes=64)
+            coef_scales = coef_mx.tile([P, G_CHUNK * POWERS * OUTPUTS], U8, align_bytes=64)
+            for values, columns in (
+                (first_powers[:].rearrange("p g n o j -> p (g n o j)"), slice(0, LAST_COLUMN)),
+                (last_power[:].rearrange("p g o j -> p (g o j)"), slice(LAST_COLUMN, None)),
+            ):
                 nc.vector.quantize_mx(
-                    out=coef_words[:, first // PACK : last // PACK].bitcast(FP8X4),
-                    scales=coef_scales[:, first // PACK : last // PACK],
-                    in_=values[:, first:last],
+                    out=coef_words[:, columns].bitcast(FP8X4),
+                    scales=coef_scales[:, columns],
+                    in_=values,
                 )
             return coef_words, coef_scales
 
@@ -165,7 +177,8 @@ def tile_kolmogorovarnoldlinear_k_kernel(
                             weight_scales = w_scales[:, group, :]
                             total = linear_sum[h]
                         else:
-                            outputs = slice((g * POWERS + n) * OUTPUTS, (g * POWERS + n + 1) * OUTPUTS)
+                            column = LAST_COLUMN + g * OUTPUTS if n == LAST else (g * LAST + n) * OUTPUTS
+                            outputs = slice(column, column + OUTPUTS)
                             weights = coef_words[:, outputs]
                             weight_scales = coef_scales[:, outputs]
                             total = basis_sum[h]
@@ -207,14 +220,11 @@ def tile_kolmogorovarnoldlinear_k_kernel(
 
         x_rows = {}
         coef_rows = {}
-        x_rows[0] = load_x(0)
-        coef_rows[0] = load_coef(0)
+        x_rows[0], coef_rows[0] = load_first_chunk()
         coef_rows[1] = load_coef(1)
         x_rows[1] = load_x(1)
         coef_rows[2] = load_coef(2)
         x_rows[2] = load_x(2)
-        coef_rows[3] = load_coef(3)
-        x_rows[3] = load_x(3)
         nc.sync.dma_start(out=balance_bf16[:], in_=pathway_balance.partition_broadcast(P))
         for quadrant in range(4):
             nc.sync.dma_start(
@@ -227,24 +237,28 @@ def tile_kolmogorovarnoldlinear_k_kernel(
             out=w_words[:].bitcast(I32),
             in_=linear_w_words.rearrange("g p o j -> p g (o j)").bitcast(I32),
         )
+        coef_rows[3] = load_coef(3)
+        x_rows[3] = load_x(3)
 
         banks = {}
         for g in range(G_CHUNK):
             banks[0, g] = turn_x(x_rows[0], g)
         last = {0: move_last(coef_rows[0])}
 
-        grouped = {0: regroup_coef(coef_rows[0]), 1: regroup_coef(coef_rows[1])}
+        grouped = {0: new_coef_grouped(), 1: new_coef_grouped()}
+        for g in range(G_CHUNK):
+            regroup_coef(coef_rows[0], grouped[0][0], slice(g, g + 1))
+        regroup_coef(coef_rows[1], grouped[1][0], slice(0, G_CHUNK))
         tiles = {0: new_activations()}
         for g in range(G_CHUNK):
             leave_psum(tiles[0], banks[0, g], g)
-        regroup_last(last[0], grouped[0])
+        regroup_last(last[0], grouped[0][1])
         last[1] = move_last(coef_rows[1])
         for g in range(G_CHUNK):
             banks[1, g] = turn_x(x_rows[1], g)
-        regroup_last(last[1], grouped[1])
+        regroup_last(last[1], grouped[1][1])
         last[2] = move_last(coef_rows[2])
-        coef = {0: quantise_coef(grouped[0]), 1: quantise_coef(grouped[1])}
-        nc.vector.tensor_copy(out=balance[:], in_=balance_bf16[:])
+        coef = {0: quantise_coef(*grouped[0]), 1: quantise_coef(*grouped[1])}
 
 
         for c in range(CHUNKS):
@@ -253,14 +267,15 @@ def tile_kolmogorovarnoldlinear_k_kernel(
                 coef_rows[c + 4] = load_coef(c + 4)
 
             if c + 2 < CHUNKS:
-                grouped[c + 2] = regroup_coef(coef_rows[c + 2])
+                grouped[c + 2] = new_coef_grouped()
+                regroup_coef(coef_rows[c + 2], grouped[c + 2][0], slice(0, G_CHUNK))
 
             now = tiles[c]
             t2_f32 = work.tile([P, G_CHUNK, ROWS * PACK], F32)
             t4_grouped = work.tile([P, G_CHUNK, ROWS * PACK], BF16, align_bytes=64)
             nc.scalar.activation(out=flat(t2_f32), in_=flat(now["t_f32"]), func=ACT.Square)
             if c + 2 < CHUNKS:
-                regroup_last(last[c + 2], grouped[c + 2])
+                regroup_last(last[c + 2], grouped[c + 2][1])
             if c + 1 < CHUNKS:
                 tiles[c + 1] = new_activations()
                 leave_psum(tiles[c + 1], banks[c + 1, 0], 0)
@@ -283,23 +298,24 @@ def tile_kolmogorovarnoldlinear_k_kernel(
                 op=ALU.mult,
             )
             if c + 2 < CHUNKS:
-                coef[c + 2] = quantise_coef(grouped[c + 2])
+                coef[c + 2] = quantise_coef(*grouped[c + 2])
             operands["t4"] = quantise(flat(t4_grouped), ("t4",))[0]
             operands["t2"], operands["t3"] = quantise(
                 t2_and_t3[:].rearrange("p a g f -> p (a g f)"), ("t2", "t3")
             )
 
             multiply(c, operands, coef[c], (("x", None), ("ones", 0), ("t", 1)))
-            if c + 3 < CHUNKS:
-                last[c + 3] = move_last(coef_rows[c + 3])
             if c + 2 < CHUNKS:
                 for g in range(G_CHUNK):
                     banks[c + 2, g] = turn_x(x_rows[c + 2], g)
+            if c + 3 < CHUNKS:
+                last[c + 3] = move_last(coef_rows[c + 3])
             multiply(c, operands, coef[c], (("t4", 4), ("t2", 2), ("t3", 3)))
 
 
         linear_part = const.tile([P, HALVES, OUTPUTS], F32)
         y = const.tile([P, HALVES, OUTPUTS], F32)
+        nc.vector.tensor_copy(out=balance[:], in_=balance_bf16[:])
         for h in range(HALVES):
             nc.scalar.activation(
                 out=linear_part[:, h, :], in_=linear_sum[h][:], func=ACT.Copy, scale=balance[:, 1:2]

@@ -25,8 +25,9 @@ G_CHUNK = 2
 K_CHUNK = G_CHUNK * K_PASS
 CHUNKS = GROUPS // G_CHUNK
 ACT_COLS = G_CHUNK * ROWS * PACK
+COEF_COLS = G_CHUNK * POWERS * OUTPUTS * PACK
+WIDEST_QUANTISE = 4096
 LAST = POWERS - 1
-LAST_COLUMN = G_CHUNK * LAST * OUTPUTS
 
 FLOPS = 2 * ROWS * FEATURES * OUTPUTS * (POWERS + 1)
 
@@ -43,71 +44,93 @@ def tile_kolmogorovarnoldlinear_k_kernel(
 
     with ExitStack() as ctx:
         const = ctx.enter_context(tc.tile_pool(name="const", bufs=1))
-        loads = ctx.enter_context(tc.tile_pool(name="loads", bufs=4))
+        loads = ctx.enter_context(tc.tile_pool(name="loads", bufs=3))
         work = ctx.enter_context(tc.tile_pool(name="work", bufs=2))
+        cubes = ctx.enter_context(tc.tile_pool(name="cubes", bufs=1))
         act_mx = ctx.enter_context(tc.tile_pool(name="act_mx", bufs=2))
         coef_mx = ctx.enter_context(tc.tile_pool(name="coef_mx", bufs=3))
         sums = ctx.enter_context(tc.psum_pool(name="sums", bufs=1))
-        turned = ctx.enter_context(tc.psum_pool(name="turned", bufs=3))
-        moved = ctx.enter_context(tc.psum_pool(name="moved", bufs=1))
+        turned_x = ctx.enter_context(tc.psum_pool(name="turned_x", bufs=G_CHUNK))
+        turned_t = ctx.enter_context(tc.psum_pool(name="turned_t", bufs=G_CHUNK * HALVES))
         ctx.enter_context(tc.manual_schedule())
 
 
-        def load_x(c):
+        def load_chunk(c, by_group):
             x_rows = loads.tile([P, G_CHUNK, HALVES, K_PASS], BF16)
+            coef_rows = loads.tile([P, G_CHUNK, PACK * OUTPUTS * POWERS], BF16)
             for g in range(G_CHUNK):
                 nc.sync.dma_start(out=x_rows[:, g, :, :], in_=x_by_group[c * G_CHUNK + g])
-            return x_rows
-
-        def load_coef(c):
-            coef_rows = loads.tile([P, G_CHUNK, PACK * OUTPUTS * POWERS], BF16)
-            nc.sync.dma_start(out=coef_rows[:], in_=coef_by_chunk[c])
-            return coef_rows
-
-        def load_first_chunk():
-            x_rows = loads.tile([P, G_CHUNK, HALVES, K_PASS], BF16)
-            coef_rows = loads.tile([P, G_CHUNK, PACK * OUTPUTS * POWERS], BF16)
-            for g in range(G_CHUNK):
-                nc.sync.dma_start(out=x_rows[:, g, :, :], in_=x_by_group[g])
-                nc.sync.dma_start(out=coef_rows[:, g, :], in_=coef_by_chunk[0][:, g, :])
+                if by_group:
+                    nc.sync.dma_start(out=coef_rows[:, g, :], in_=coef_by_chunk[c][:, g, :])
+            if not by_group:
+                nc.sync.dma_start(out=coef_rows[:], in_=coef_by_chunk[c])
             return x_rows, coef_rows
 
-        def turn_x(x_rows, g):
-            x_words = x_rows[:, g, :, :].bitcast(F32)
-            bank = turned.tile([P, 2, ROWS], F32)
-            for u in range(2):
+        def tanh_rows(x_rows, pieces):
+            t_rows = work.tile([P, G_CHUNK, HALVES, K_PASS], F32)
+            width = G_CHUNK // pieces
+            for i in range(pieces):
+                groups = slice(i * width, (i + 1) * width)
+                nc.scalar.activation(
+                    out=t_rows[:, groups, :, :].rearrange("p g h k -> p (g h k)"),
+                    in_=x_rows[:, groups, :, :].rearrange("p g h k -> p (g h k)"),
+                    func=ACT.Tanh,
+                )
+            return t_rows
+
+        def turn_x(x_rows):
+            x_words = x_rows[:].rearrange("p g h k -> p (g h k)").bitcast(F32)
+            banks = []
+            for g in range(G_CHUNK):
+                bank = turned_x.tile([P, 2, ROWS], F32)
+                for u in range(2):
+                    for h in range(HALVES):
+                        first = (g * HALVES + h) * 2 * P
+                        nc.tensor.transpose(
+                            bank[:, u, h * P : (h + 1) * P],
+                            x_words[:, first + u : first + 2 * P : 2],
+                            identity[:],
+                        )
+                banks.append(bank)
+            return banks
+
+        def turn_t(t_rows):
+            banks = []
+            for g in range(G_CHUNK):
                 for h in range(HALVES):
-                    nc.tensor.transpose(
-                        bank[:, u, h * P : (h + 1) * P],
-                        x_words[:, h, u : 2 * P : 2],
-                        identity[:],
-                    )
-            return bank
+                    t_bank = turned_t.tile([P, PACK, P], F32)
+                    for j in range(PACK):
+                        nc.tensor.transpose(
+                            t_bank[:, j, :], t_rows[:, g, h, j : K_PASS : PACK], identity[:]
+                        )
+                    banks.append(t_bank)
+            return banks
 
-        def new_activations():
-            x_and_t = work.tile([P, 2, G_CHUNK, ROWS * PACK], BF16, align_bytes=64)
-            t_f32 = work.tile([P, G_CHUNK, ROWS * PACK], F32)
-            return {"x_and_t": x_and_t, "t_f32": t_f32}
+        def x_out(x_and_t, banks):
+            for g in range(G_CHUNK):
+                nc.scalar.copy(
+                    out=x_and_t[:, 0, g, :].bitcast(F32).rearrange("p (r u) -> p r u", u=2),
+                    in_=banks[g][:].rearrange("p u r -> p r u"),
+                )
 
-        def leave_psum(tiles, bank, g):
-            nc.scalar.copy(
-                out=tiles["x_and_t"][:, 0, g, :].bitcast(F32).rearrange("p (r u) -> p r u", u=2),
-                in_=bank[:].rearrange("p u r -> p r u"),
-            )
-            x_values = bank[:].bitcast(BF16).rearrange("p u (r e) -> p r u e", e=2)
-            nc.scalar.activation(
-                out=tiles["t_f32"][:, g, :].rearrange("p (r u e) -> p r u e", u=2, e=2),
-                in_=x_values,
-                func=ACT.Tanh,
-            )
-            nc.scalar.activation(
-                out=tiles["x_and_t"][:, 1, g, :].rearrange("p (r u e) -> p r u e", u=2, e=2),
-                in_=x_values,
-                func=ACT.Tanh,
-            )
+        def by_word(bank):
+            return bank[:].rearrange("p j r -> p r j")
 
-        def flat(tile):
-            return tile[:].rearrange("p g f -> p (g f)")
+        def piece(tile, i):
+            return tile[:, i * P * PACK : (i + 1) * P * PACK].rearrange("p (r j) -> p r j", j=PACK)
+
+        def square_and_round(x_and_t, banks):
+            t2_f32 = work.tile([P, ACT_COLS], F32)
+            t_bf16 = x_and_t[:, 1, :, :].rearrange("p g f -> p (g f)")
+            for i, bank in enumerate(banks):
+                nc.scalar.activation(out=piece(t2_f32, i), in_=by_word(bank), func=ACT.Square)
+                nc.scalar.copy(out=piece(t_bf16, i), in_=by_word(bank))
+            return t2_f32
+
+        def fourth_power(t2_f32):
+            t4 = work.tile([P, ACT_COLS], BF16, align_bytes=64)
+            nc.scalar.activation(out=t4[:], in_=t2_f32[:], func=ACT.Square)
+            return t4
 
         def quantise(values, names):
             columns = len(names) * ACT_COLS // PACK
@@ -116,50 +139,33 @@ def tile_kolmogorovarnoldlinear_k_kernel(
             nc.vector.quantize_mx(out=words[:].bitcast(FP8X4), scales=scales[:], in_=values)
             return [(words, scales, i * ACT_COLS // PACK) for i in range(len(names))]
 
-        def new_coef_grouped():
-            first_powers = work.tile([P, G_CHUNK, LAST, OUTPUTS, PACK], BF16, align_bytes=64)
-            last_power = work.tile([P, G_CHUNK, OUTPUTS, PACK], BF16, align_bytes=64)
-            return first_powers, last_power
-
-        def regroup_coef(coef_rows, first_powers, groups):
+        def regroup_coef(coef_rows, pieces):
+            coef_grouped = work.tile([P, G_CHUNK, POWERS, OUTPUTS, PACK], BF16, align_bytes=64)
             by_output_in = coef_rows[:].rearrange(
                 "p g (j o n) -> p g o n j", j=PACK, o=OUTPUTS, n=POWERS
             )
-            by_output_out = first_powers[:].rearrange("p g n o j -> p g o n j")
-            nc.vector.tensor_copy(
-                out=by_output_out[:, groups, :, :, :], in_=by_output_in[:, groups, :, 0:LAST, :]
-            )
-
-        def move_last(coef_rows):
-            bank = moved.tile([P, G_CHUNK, OUTPUTS, PACK], BF16)
-            by_power = coef_rows[:].rearrange("p g (j o n) -> p g n o j", j=PACK, o=OUTPUTS, n=POWERS)
-            for g in range(G_CHUNK):
-                nc.tensor.matmul(
-                    out=bank[:, g, :, :],
-                    lhsT=identity_bf16[:],
-                    rhs=by_power[:, g, LAST, :, :],
-                    start=True,
-                    stop=True,
+            by_output_out = coef_grouped[:].rearrange("p g n o j -> p g o n j")
+            width = G_CHUNK // pieces
+            for i in range(pieces):
+                groups = slice(i * width, (i + 1) * width)
+                nc.vector.tensor_copy(
+                    out=by_output_out[:, groups, :, 0:LAST, :], in_=by_output_in[:, groups, :, 0:LAST, :]
                 )
-            return bank
+                nc.vector.tensor_copy(
+                    out=by_output_out[:, groups, :, LAST, :], in_=by_output_in[:, groups, :, LAST, :]
+                )
+            return coef_grouped
 
-        def regroup_last(bank, last_power):
-            nc.scalar.copy(
-                out=last_power[:].rearrange("p g o j -> p (g o j)"),
-                in_=bank[:].rearrange("p g o j -> p (g o j)"),
-            )
-
-        def quantise_coef(first_powers, last_power):
-            coef_words = coef_mx.tile([P, G_CHUNK * POWERS * OUTPUTS], U32, align_bytes=64)
-            coef_scales = coef_mx.tile([P, G_CHUNK * POWERS * OUTPUTS], U8, align_bytes=64)
-            for values, columns in (
-                (first_powers[:].rearrange("p g n o j -> p (g n o j)"), slice(0, LAST_COLUMN)),
-                (last_power[:].rearrange("p g o j -> p (g o j)"), slice(LAST_COLUMN, None)),
-            ):
+        def quantise_coef(coef_grouped):
+            coef_words = coef_mx.tile([P, COEF_COLS // PACK], U32, align_bytes=64)
+            coef_scales = coef_mx.tile([P, COEF_COLS // PACK], U8, align_bytes=64)
+            values = coef_grouped[:].rearrange("p g n o j -> p (g n o j)")
+            for first in range(0, COEF_COLS, WIDEST_QUANTISE):
+                last = min(first + WIDEST_QUANTISE, COEF_COLS)
                 nc.vector.quantize_mx(
-                    out=coef_words[:, columns].bitcast(FP8X4),
-                    scales=coef_scales[:, columns],
-                    in_=values,
+                    out=coef_words[:, first // PACK : last // PACK].bitcast(FP8X4),
+                    scales=coef_scales[:, first // PACK : last // PACK],
+                    in_=values[:, first:last],
                 )
             return coef_words, coef_scales
 
@@ -169,28 +175,26 @@ def tile_kolmogorovarnoldlinear_k_kernel(
                 words, scales, first_column = operands[name]
                 for g in range(G_CHUNK):
                     group = c * G_CHUNK + g
-                    for h in range(HALVES):
-                        first_row = first_column if name == "ones" else first_column + (g * HALVES + h) * P
-                        rows = slice(first_row, first_row + P)
-                        if name == "x":
-                            weights = w_words[:, group, :]
-                            weight_scales = w_scales[:, group, :]
-                            total = linear_sum[h]
-                        else:
-                            column = LAST_COLUMN + g * OUTPUTS if n == LAST else (g * LAST + n) * OUTPUTS
-                            outputs = slice(column, column + OUTPUTS)
-                            weights = coef_words[:, outputs]
-                            weight_scales = coef_scales[:, outputs]
-                            total = basis_sum[h]
-                        nc.tensor.matmul_mx(
-                            out=total[:],
-                            lhsT=words[:, rows].bitcast(FP8X4),
-                            lhsT_scale=scales[:, rows],
-                            rhs=weights.bitcast(FP8X4),
-                            rhs_scale=weight_scales,
-                            start=(group == 0 and name in ("x", "ones")),
-                            stop=(group == GROUPS - 1 and name in ("x", "t3")),
-                        )
+                    first_row = first_column if name == "ones" else first_column + g * ROWS
+                    rows = slice(first_row, first_row + ROWS)
+                    if name == "x":
+                        weights = w_words[:, group, :]
+                        weight_scales = w_scales[:, group, :]
+                        total = linear_sum
+                    else:
+                        outputs = slice((g * POWERS + n) * OUTPUTS, (g * POWERS + n + 1) * OUTPUTS)
+                        weights = coef_words[:, outputs]
+                        weight_scales = coef_scales[:, outputs]
+                        total = basis_sum
+                    nc.tensor.matmul_mx(
+                        out=total[:],
+                        lhsT=weights.bitcast(FP8X4),
+                        lhsT_scale=weight_scales,
+                        rhs=words[:, rows].bitcast(FP8X4),
+                        rhs_scale=scales[:, rows],
+                        start=(group == 0 and name in ("x", "ones")),
+                        stop=(group == GROUPS - 1 and name in ("x", "t3")),
+                    )
 
 
         warm = const.tile([P, 1], F32)
@@ -199,13 +203,11 @@ def tile_kolmogorovarnoldlinear_k_kernel(
 
         identity = const.tile([P, P], F32)
         make_identity(nc, identity[:])
-        identity_bf16 = const.tile([P, P], BF16)
-        make_identity(nc, identity_bf16[:])
 
-        ones = const.tile([P, P * PACK], BF16, align_bytes=64)
+        ones = const.tile([P, ROWS * PACK], BF16, align_bytes=64)
         nc.vector.memset(ones[:], 1.0)
-        ones_words = const.tile([P, P], U32, align_bytes=64)
-        ones_scales = const.tile([P, P], U8, align_bytes=64)
+        ones_words = const.tile([P, ROWS], U32, align_bytes=64)
+        ones_scales = const.tile([P, ROWS], U8, align_bytes=64)
         nc.vector.quantize_mx(out=ones_words[:].bitcast(FP8X4), scales=ones_scales[:], in_=ones[:])
 
         w_scales = const.tile([P, GROUPS, OUTPUTS], U8, align_bytes=64)
@@ -214,17 +216,11 @@ def tile_kolmogorovarnoldlinear_k_kernel(
         balance_bf16 = const.tile([P, 2], BF16)
         balance = const.tile([P, 2], F32)
 
-        basis_sum = [sums.tile([P, OUTPUTS], F32, name="basis_sum%d" % h) for h in range(HALVES)]
-        linear_sum = [sums.tile([P, OUTPUTS], F32, name="linear_sum%d" % h) for h in range(HALVES)]
+        basis_sum = sums.tile([OUTPUTS, ROWS], F32)
+        linear_sum = sums.tile([OUTPUTS, ROWS], F32)
 
 
-        x_rows = {}
-        coef_rows = {}
-        x_rows[0], coef_rows[0] = load_first_chunk()
-        coef_rows[1] = load_coef(1)
-        x_rows[1] = load_x(1)
-        coef_rows[2] = load_coef(2)
-        x_rows[2] = load_x(2)
+        loaded = {0: load_chunk(0, True), 1: load_chunk(1, False), 2: load_chunk(2, False)}
         nc.sync.dma_start(out=balance_bf16[:], in_=pathway_balance.partition_broadcast(P))
         for quadrant in range(4):
             nc.sync.dma_start(
@@ -237,96 +233,89 @@ def tile_kolmogorovarnoldlinear_k_kernel(
             out=w_words[:].bitcast(I32),
             in_=linear_w_words.rearrange("g p o j -> p g (o j)").bitcast(I32),
         )
-        coef_rows[3] = load_coef(3)
-        x_rows[3] = load_x(3)
 
-        banks = {}
-        for g in range(G_CHUNK):
-            banks[0, g] = turn_x(x_rows[0], g)
-        last = {0: move_last(coef_rows[0])}
-
-        grouped = {0: new_coef_grouped(), 1: new_coef_grouped()}
-        for g in range(G_CHUNK):
-            regroup_coef(coef_rows[0], grouped[0][0], slice(g, g + 1))
-        regroup_coef(coef_rows[1], grouped[1][0], slice(0, G_CHUNK))
-        tiles = {0: new_activations()}
-        for g in range(G_CHUNK):
-            leave_psum(tiles[0], banks[0, g], g)
-        regroup_last(last[0], grouped[0][1])
-        last[1] = move_last(coef_rows[1])
-        for g in range(G_CHUNK):
-            banks[1, g] = turn_x(x_rows[1], g)
-        regroup_last(last[1], grouped[1][1])
-        last[2] = move_last(coef_rows[2])
-        coef = {0: quantise_coef(*grouped[0]), 1: quantise_coef(*grouped[1])}
+        grouped = {}
+        coef = {}
+        t_rows = {0: tanh_rows(loaded[0][0], G_CHUNK)}
+        t_banks = {0: turn_t(t_rows[0])}
+        x_banks = {0: turn_x(loaded[0][0])}
+        grouped[0] = regroup_coef(loaded[0][1], G_CHUNK)
+        x_and_t = {0: work.tile([P, 2, G_CHUNK, ROWS * PACK], BF16, name="x_and_t", align_bytes=64)}
+        t_rows[1] = tanh_rows(loaded[1][0], 1)
+        grouped[1] = regroup_coef(loaded[1][1], 1)
+        t2_f32 = {0: square_and_round(x_and_t[0], t_banks[0])}
+        x_out(x_and_t[0], x_banks[0])
+        x_banks[1] = turn_x(loaded[1][0])
+        t4 = {0: fourth_power(t2_f32[0])}
+        coef[0] = quantise_coef(grouped[0])
+        coef[1] = quantise_coef(grouped[1])
 
 
         for c in range(CHUNKS):
-            if c + 4 < CHUNKS:
-                x_rows[c + 4] = load_x(c + 4)
-                coef_rows[c + 4] = load_coef(c + 4)
-
-            if c + 2 < CHUNKS:
-                grouped[c + 2] = new_coef_grouped()
-                regroup_coef(coef_rows[c + 2], grouped[c + 2][0], slice(0, G_CHUNK))
-
-            now = tiles[c]
-            t2_f32 = work.tile([P, G_CHUNK, ROWS * PACK], F32)
-            t4_grouped = work.tile([P, G_CHUNK, ROWS * PACK], BF16, align_bytes=64)
-            nc.scalar.activation(out=flat(t2_f32), in_=flat(now["t_f32"]), func=ACT.Square)
-            if c + 2 < CHUNKS:
-                regroup_last(last[c + 2], grouped[c + 2][1])
-            if c + 1 < CHUNKS:
-                tiles[c + 1] = new_activations()
-                leave_psum(tiles[c + 1], banks[c + 1, 0], 0)
-            nc.scalar.activation(out=flat(t4_grouped), in_=flat(t2_f32), func=ACT.Square)
-            if c + 1 < CHUNKS:
-                leave_psum(tiles[c + 1], banks[c + 1, 1], 1)
-
-            operands = {"ones": (ones_words, ones_scales, 0)}
-            operands["x"], operands["t"] = quantise(
-                now["x_and_t"][:].rearrange("p a g f -> p (a g f)"), ("x", "t")
-            )
-            t2_and_t3 = work.tile([P, 2, G_CHUNK, ROWS * PACK], BF16, align_bytes=64)
-            nc.vector.tensor_copy(
-                out=t2_and_t3[:, 0, :, :].rearrange("p g f -> p (g f)"), in_=flat(t2_f32)
-            )
-            nc.vector.tensor_tensor(
-                out=t2_and_t3[:, 1, :, :].rearrange("p g f -> p (g f)"),
-                in0=flat(t2_f32),
-                in1=flat(now["t_f32"]),
-                op=ALU.mult,
-            )
-            if c + 2 < CHUNKS:
-                coef[c + 2] = quantise_coef(*grouped[c + 2])
-            operands["t4"] = quantise(flat(t4_grouped), ("t4",))[0]
-            operands["t2"], operands["t3"] = quantise(
-                t2_and_t3[:].rearrange("p a g f -> p (a g f)"), ("t2", "t3")
-            )
-
-            multiply(c, operands, coef[c], (("x", None), ("ones", 0), ("t", 1)))
-            if c + 2 < CHUNKS:
-                for g in range(G_CHUNK):
-                    banks[c + 2, g] = turn_x(x_rows[c + 2], g)
             if c + 3 < CHUNKS:
-                last[c + 3] = move_last(coef_rows[c + 3])
-            multiply(c, operands, coef[c], (("t4", 4), ("t2", 2), ("t3", 3)))
+                loaded[c + 3] = load_chunk(c + 3, False)
 
-
-        linear_part = const.tile([P, HALVES, OUTPUTS], F32)
-        y = const.tile([P, HALVES, OUTPUTS], F32)
-        nc.vector.tensor_copy(out=balance[:], in_=balance_bf16[:])
-        for h in range(HALVES):
-            nc.scalar.activation(
-                out=linear_part[:, h, :], in_=linear_sum[h][:], func=ACT.Copy, scale=balance[:, 1:2]
-            )
-        for h in range(HALVES):
-            nc.vector.scalar_tensor_tensor(
-                out=y[:, h, :],
-                in0=basis_sum[h][:],
-                scalar=balance[:, 0:1],
-                in1=linear_part[:, h, :],
+            t2_and_t3 = cubes.tile([P, 2, ACT_COLS], BF16, align_bytes=64)
+            nc.gpsimd.tensor_scalar(
+                out=t2_and_t3[:, 0, :],
+                in0=t2_f32[c][:],
+                scalar1=1.0,
+                scalar2=0.0,
                 op0=ALU.mult,
                 op1=ALU.add,
             )
+            for i, bank in enumerate(t_banks[c]):
+                nc.vector.tensor_tensor(
+                    out=piece(t2_and_t3[:, 1, :], i),
+                    in0=piece(t2_f32[c], i),
+                    in1=by_word(bank),
+                    op=ALU.mult,
+                )
+            if c + 1 < CHUNKS:
+                t_banks[c + 1] = turn_t(t_rows[c + 1])
+
+            if c + 2 < CHUNKS:
+                t_rows[c + 2] = tanh_rows(loaded[c + 2][0], 1)
+            if c + 1 < CHUNKS:
+                x_and_t[c + 1] = work.tile(
+                    [P, 2, G_CHUNK, ROWS * PACK], BF16, name="x_and_t", align_bytes=64
+                )
+                x_out(x_and_t[c + 1], x_banks[c + 1])
+                t2_f32[c + 1] = square_and_round(x_and_t[c + 1], t_banks[c + 1])
+                t4[c + 1] = fourth_power(t2_f32[c + 1])
+
+            if c + 2 < CHUNKS:
+                grouped[c + 2] = regroup_coef(loaded[c + 2][1], 1)
+            operands = {"ones": (ones_words, ones_scales, 0)}
+            operands["x"], operands["t"] = quantise(
+                x_and_t[c][:].rearrange("p a g f -> p (a g f)"), ("x", "t")
+            )
+            multiply(c, operands, coef[c], (("x", None), ("ones", 0), ("t", 1)))
+            if c + 2 < CHUNKS:
+                x_banks[c + 2] = turn_x(loaded[c + 2][0])
+                coef[c + 2] = quantise_coef(grouped[c + 2])
+            operands["t4"] = quantise(t4[c][:], ("t4",))[0]
+            operands["t2"], operands["t3"] = quantise(
+                t2_and_t3[:].rearrange("p a f -> p (a f)"), ("t2", "t3")
+            )
+            multiply(c, operands, coef[c], (("t4", 4), ("t2", 2), ("t3", 3)))
+
+
+        nc.vector.tensor_copy(out=balance[:], in_=balance_bf16[:])
+        linear_part = const.tile([OUTPUTS, ROWS], F32)
+        y_turned = const.tile([OUTPUTS, ROWS], F32)
+        y = const.tile([P, HALVES, OUTPUTS], F32)
+        nc.scalar.activation(out=linear_part[:], in_=linear_sum[:], func=ACT.Copy, scale=balance[:, 1:2])
+        nc.vector.scalar_tensor_tensor(
+            out=y_turned[:],
+            in0=basis_sum[:],
+            scalar=balance[:, 0:1],
+            in1=linear_part[:],
+            op0=ALU.mult,
+            op1=ALU.add,
+        )
+        for h in range(HALVES):
+            y_bank = turned_x.tile([P, 2, ROWS], F32, name="bank")
+            nc.tensor.transpose(y_bank[:, 0, 0:OUTPUTS], y_turned[:, h * P : (h + 1) * P], identity[:])
+            nc.vector.tensor_copy(out=y[:, h, :], in_=y_bank[:, 0, 0:OUTPUTS])
             nc.sync.dma_start(out=out[h], in_=y[:, h, :])

@@ -27,7 +27,7 @@ CHUNKS = GROUPS // G_CHUNK
 ACT_COLS = G_CHUNK * ROWS * PACK
 COEF_COLS = G_CHUNK * POWERS * OUTPUTS * PACK
 WIDEST_QUANTISE = 4096
-LAST = POWERS - 1
+SPLIT = 3
 
 FLOPS = 2 * ROWS * FEATURES * OUTPUTS * (POWERS + 1)
 
@@ -46,7 +46,7 @@ def tile_kolmogorovarnoldlinear_k_kernel(
         const = ctx.enter_context(tc.tile_pool(name="const", bufs=1))
         loads = ctx.enter_context(tc.tile_pool(name="loads", bufs=3))
         work = ctx.enter_context(tc.tile_pool(name="work", bufs=2))
-        cubes = ctx.enter_context(tc.tile_pool(name="cubes", bufs=1))
+        squares = ctx.enter_context(tc.tile_pool(name="squares", bufs=1))
         act_mx = ctx.enter_context(tc.tile_pool(name="act_mx", bufs=2))
         coef_mx = ctx.enter_context(tc.tile_pool(name="coef_mx", bufs=3))
         sums = ctx.enter_context(tc.psum_pool(name="sums", bufs=1))
@@ -58,12 +58,12 @@ def tile_kolmogorovarnoldlinear_k_kernel(
         def load_chunk(c, by_group):
             x_rows = loads.tile([P, G_CHUNK, HALVES, K_PASS], BF16)
             coef_rows = loads.tile([P, G_CHUNK, PACK * OUTPUTS * POWERS], BF16)
+            if not by_group:
+                nc.sync.dma_start(out=coef_rows[:], in_=coef_by_chunk[c])
             for g in range(G_CHUNK):
                 nc.sync.dma_start(out=x_rows[:, g, :, :], in_=x_by_group[c * G_CHUNK + g])
                 if by_group:
                     nc.sync.dma_start(out=coef_rows[:, g, :], in_=coef_by_chunk[c][:, g, :])
-            if not by_group:
-                nc.sync.dma_start(out=coef_rows[:], in_=coef_by_chunk[c])
             return x_rows, coef_rows
 
         def tanh_rows(x_rows, pieces):
@@ -128,9 +128,9 @@ def tile_kolmogorovarnoldlinear_k_kernel(
             return t2_f32
 
         def fourth_power(t2_f32):
-            t4 = work.tile([P, ACT_COLS], BF16, align_bytes=64)
-            nc.scalar.activation(out=t4[:], in_=t2_f32[:], func=ACT.Square)
-            return t4
+            t3_and_t4 = work.tile([P, 2, ACT_COLS], BF16, align_bytes=64)
+            nc.scalar.activation(out=t3_and_t4[:, 1, :], in_=t2_f32[:], func=ACT.Square)
+            return t3_and_t4
 
         def quantise(values, names):
             columns = len(names) * ACT_COLS // PACK
@@ -148,12 +148,11 @@ def tile_kolmogorovarnoldlinear_k_kernel(
             width = G_CHUNK // pieces
             for i in range(pieces):
                 groups = slice(i * width, (i + 1) * width)
-                nc.vector.tensor_copy(
-                    out=by_output_out[:, groups, :, 0:LAST, :], in_=by_output_in[:, groups, :, 0:LAST, :]
-                )
-                nc.vector.tensor_copy(
-                    out=by_output_out[:, groups, :, LAST, :], in_=by_output_in[:, groups, :, LAST, :]
-                )
+                for powers in (slice(0, SPLIT), slice(SPLIT, POWERS)):
+                    nc.vector.tensor_copy(
+                        out=by_output_out[:, groups, :, powers, :],
+                        in_=by_output_in[:, groups, :, powers, :],
+                    )
             return coef_grouped
 
         def quantise_coef(coef_grouped):
@@ -193,7 +192,7 @@ def tile_kolmogorovarnoldlinear_k_kernel(
                         rhs=words[:, rows].bitcast(FP8X4),
                         rhs_scale=scales[:, rows],
                         start=(group == 0 and name in ("x", "ones")),
-                        stop=(group == GROUPS - 1 and name in ("x", "t3")),
+                        stop=(group == GROUPS - 1 and name in ("x", "t4")),
                     )
 
 
@@ -241,23 +240,25 @@ def tile_kolmogorovarnoldlinear_k_kernel(
         x_banks = {0: turn_x(loaded[0][0])}
         grouped[0] = regroup_coef(loaded[0][1], G_CHUNK)
         x_and_t = {0: work.tile([P, 2, G_CHUNK, ROWS * PACK], BF16, name="x_and_t", align_bytes=64)}
-        t_rows[1] = tanh_rows(loaded[1][0], 1)
+        coef[0] = quantise_coef(grouped[0])
         grouped[1] = regroup_coef(loaded[1][1], 1)
         t2_f32 = {0: square_and_round(x_and_t[0], t_banks[0])}
         x_out(x_and_t[0], x_banks[0])
+        t_rows[1] = tanh_rows(loaded[1][0], 1)
         x_banks[1] = turn_x(loaded[1][0])
-        t4 = {0: fourth_power(t2_f32[0])}
-        coef[0] = quantise_coef(grouped[0])
+        t3_and_t4 = {0: fourth_power(t2_f32[0])}
         coef[1] = quantise_coef(grouped[1])
+
+        nc.gpsimd.tensor_copy(out=balance[:], in_=balance_bf16[:])
 
 
         for c in range(CHUNKS):
             if c + 3 < CHUNKS:
                 loaded[c + 3] = load_chunk(c + 3, False)
 
-            t2_and_t3 = cubes.tile([P, 2, ACT_COLS], BF16, align_bytes=64)
+            t2 = squares.tile([P, ACT_COLS], BF16, align_bytes=64)
             nc.gpsimd.tensor_scalar(
-                out=t2_and_t3[:, 0, :],
+                out=t2[:],
                 in0=t2_f32[c][:],
                 scalar1=1.0,
                 scalar2=0.0,
@@ -266,7 +267,7 @@ def tile_kolmogorovarnoldlinear_k_kernel(
             )
             for i, bank in enumerate(t_banks[c]):
                 nc.vector.tensor_tensor(
-                    out=piece(t2_and_t3[:, 1, :], i),
+                    out=piece(t3_and_t4[c][:, 0, :], i),
                     in0=piece(t2_f32[c], i),
                     in1=by_word(bank),
                     op=ALU.mult,
@@ -282,7 +283,7 @@ def tile_kolmogorovarnoldlinear_k_kernel(
                 )
                 x_out(x_and_t[c + 1], x_banks[c + 1])
                 t2_f32[c + 1] = square_and_round(x_and_t[c + 1], t_banks[c + 1])
-                t4[c + 1] = fourth_power(t2_f32[c + 1])
+                t3_and_t4[c + 1] = fourth_power(t2_f32[c + 1])
 
             if c + 2 < CHUNKS:
                 grouped[c + 2] = regroup_coef(loaded[c + 2][1], 1)
@@ -294,14 +295,13 @@ def tile_kolmogorovarnoldlinear_k_kernel(
             if c + 2 < CHUNKS:
                 x_banks[c + 2] = turn_x(loaded[c + 2][0])
                 coef[c + 2] = quantise_coef(grouped[c + 2])
-            operands["t4"] = quantise(t4[c][:], ("t4",))[0]
-            operands["t2"], operands["t3"] = quantise(
-                t2_and_t3[:].rearrange("p a f -> p (a f)"), ("t2", "t3")
+            operands["t2"] = quantise(t2[:], ("t2",))[0]
+            operands["t3"], operands["t4"] = quantise(
+                t3_and_t4[c][:].rearrange("p a f -> p (a f)"), ("t3", "t4")
             )
-            multiply(c, operands, coef[c], (("t4", 4), ("t2", 2), ("t3", 3)))
+            multiply(c, operands, coef[c], (("t2", 2), ("t3", 3), ("t4", 4)))
 
 
-        nc.vector.tensor_copy(out=balance[:], in_=balance_bf16[:])
         linear_part = const.tile([OUTPUTS, ROWS], F32)
         y_turned = const.tile([OUTPUTS, ROWS], F32)
         y = const.tile([P, HALVES, OUTPUTS], F32)

@@ -55,16 +55,19 @@ def tile_kolmogorovarnoldlinear_k_kernel(
         ctx.enter_context(tc.manual_schedule())
 
 
-        def load_chunk(c, by_group):
+        def load_x(c):
             x_rows = loads.tile([P, G_CHUNK, HALVES, K_PASS], BF16)
-            coef_rows = loads.tile([P, G_CHUNK, PACK * OUTPUTS * POWERS], BF16)
-            if not by_group:
-                nc.sync.dma_start(out=coef_rows[:], in_=coef_by_chunk[c])
             for g in range(G_CHUNK):
                 nc.sync.dma_start(out=x_rows[:, g, :, :], in_=x_by_group[c * G_CHUNK + g])
-                if by_group:
-                    nc.sync.dma_start(out=coef_rows[:, g, :], in_=coef_by_chunk[c][:, g, :])
-            return x_rows, coef_rows
+            return x_rows
+
+        def load_coef(c, pieces):
+            coef_rows = loads.tile([P, G_CHUNK, PACK * OUTPUTS * POWERS], BF16)
+            width = G_CHUNK // pieces
+            for i in range(pieces):
+                groups = slice(i * width, (i + 1) * width)
+                nc.sync.dma_start(out=coef_rows[:, groups, :], in_=coef_by_chunk[c][:, groups, :])
+            return coef_rows
 
         def tanh_rows(x_rows, pieces):
             t_rows = work.tile([P, G_CHUNK, HALVES, K_PASS], F32)
@@ -119,13 +122,16 @@ def tile_kolmogorovarnoldlinear_k_kernel(
         def piece(tile, i):
             return tile[:, i * P * PACK : (i + 1) * P * PACK].rearrange("p (r j) -> p r j", j=PACK)
 
-        def square_and_round(x_and_t, banks):
+        def square(banks):
             t2_f32 = work.tile([P, ACT_COLS], F32)
-            t_bf16 = x_and_t[:, 1, :, :].rearrange("p g f -> p (g f)")
             for i, bank in enumerate(banks):
                 nc.scalar.activation(out=piece(t2_f32, i), in_=by_word(bank), func=ACT.Square)
-                nc.scalar.copy(out=piece(t_bf16, i), in_=by_word(bank))
             return t2_f32
+
+        def round_t(x_and_t, banks):
+            t_bf16 = x_and_t[:, 1, :, :].rearrange("p g f -> p (g f)")
+            for i, bank in enumerate(banks):
+                nc.scalar.copy(out=piece(t_bf16, i), in_=by_word(bank))
 
         def fourth_power(t2_f32):
             t3_and_t4 = work.tile([P, 2, ACT_COLS], BF16, align_bytes=64)
@@ -139,19 +145,17 @@ def tile_kolmogorovarnoldlinear_k_kernel(
             nc.vector.quantize_mx(out=words[:].bitcast(FP8X4), scales=scales[:], in_=values)
             return [(words, scales, i * ACT_COLS // PACK) for i in range(len(names))]
 
-        def regroup_coef(coef_rows, pieces):
+        def regroup_coef(coef_rows):
             coef_grouped = work.tile([P, G_CHUNK, POWERS, OUTPUTS, PACK], BF16, align_bytes=64)
             by_output_in = coef_rows[:].rearrange(
-                "p g (j o n) -> p g o n j", j=PACK, o=OUTPUTS, n=POWERS
+                "p g (a b o n) -> p g o a n b", a=PACK // 2, b=2, o=OUTPUTS, n=POWERS
             )
-            by_output_out = coef_grouped[:].rearrange("p g n o j -> p g o n j")
-            width = G_CHUNK // pieces
-            for i in range(pieces):
-                groups = slice(i * width, (i + 1) * width)
+            by_output_out = coef_grouped[:].rearrange("p g n o (a b) -> p g o a n b", b=2)
+            for g in range(G_CHUNK):
                 for powers in (slice(0, SPLIT), slice(SPLIT, POWERS)):
                     nc.vector.tensor_copy(
-                        out=by_output_out[:, groups, :, powers, :],
-                        in_=by_output_in[:, groups, :, powers, :],
+                        out=by_output_out[:, g, :, :, powers, :],
+                        in_=by_output_in[:, g, :, :, powers, :],
                     )
             return coef_grouped
 
@@ -219,7 +223,11 @@ def tile_kolmogorovarnoldlinear_k_kernel(
         linear_sum = sums.tile([OUTPUTS, ROWS], F32)
 
 
-        loaded = {0: load_chunk(0, True), 1: load_chunk(1, False), 2: load_chunk(2, False)}
+        x_rows = {0: load_x(0)}
+        coef_rows = {0: load_coef(0, G_CHUNK), 1: load_coef(1, 1)}
+        x_rows[1] = load_x(1)
+        coef_rows[2] = load_coef(2, 1)
+        x_rows[2] = load_x(2)
         nc.sync.dma_start(out=balance_bf16[:], in_=pathway_balance.partition_broadcast(P))
         for quadrant in range(4):
             nc.sync.dma_start(
@@ -235,17 +243,18 @@ def tile_kolmogorovarnoldlinear_k_kernel(
 
         grouped = {}
         coef = {}
-        t_rows = {0: tanh_rows(loaded[0][0], G_CHUNK)}
+        t_rows = {0: tanh_rows(x_rows[0], G_CHUNK)}
         t_banks = {0: turn_t(t_rows[0])}
-        x_banks = {0: turn_x(loaded[0][0])}
-        grouped[0] = regroup_coef(loaded[0][1], G_CHUNK)
+        x_banks = {0: turn_x(x_rows[0])}
+        grouped[0] = regroup_coef(coef_rows[0])
         x_and_t = {0: work.tile([P, 2, G_CHUNK, ROWS * PACK], BF16, name="x_and_t", align_bytes=64)}
         coef[0] = quantise_coef(grouped[0])
-        grouped[1] = regroup_coef(loaded[1][1], 1)
-        t2_f32 = {0: square_and_round(x_and_t[0], t_banks[0])}
+        grouped[1] = regroup_coef(coef_rows[1])
+        t2_f32 = {0: square(t_banks[0])}
+        round_t(x_and_t[0], t_banks[0])
         x_out(x_and_t[0], x_banks[0])
-        t_rows[1] = tanh_rows(loaded[1][0], 1)
-        x_banks[1] = turn_x(loaded[1][0])
+        t_rows[1] = tanh_rows(x_rows[1], 1)
+        x_banks[1] = turn_x(x_rows[1])
         t3_and_t4 = {0: fourth_power(t2_f32[0])}
         coef[1] = quantise_coef(grouped[1])
 
@@ -254,7 +263,8 @@ def tile_kolmogorovarnoldlinear_k_kernel(
 
         for c in range(CHUNKS):
             if c + 3 < CHUNKS:
-                loaded[c + 3] = load_chunk(c + 3, False)
+                coef_rows[c + 3] = load_coef(c + 3, 1)
+                x_rows[c + 3] = load_x(c + 3)
 
             t2 = squares.tile([P, ACT_COLS], BF16, align_bytes=64)
             nc.gpsimd.tensor_scalar(
@@ -276,24 +286,25 @@ def tile_kolmogorovarnoldlinear_k_kernel(
                 t_banks[c + 1] = turn_t(t_rows[c + 1])
 
             if c + 2 < CHUNKS:
-                t_rows[c + 2] = tanh_rows(loaded[c + 2][0], 1)
+                t_rows[c + 2] = tanh_rows(x_rows[c + 2], 1)
             if c + 1 < CHUNKS:
                 x_and_t[c + 1] = work.tile(
                     [P, 2, G_CHUNK, ROWS * PACK], BF16, name="x_and_t", align_bytes=64
                 )
                 x_out(x_and_t[c + 1], x_banks[c + 1])
-                t2_f32[c + 1] = square_and_round(x_and_t[c + 1], t_banks[c + 1])
+                t2_f32[c + 1] = square(t_banks[c + 1])
+                round_t(x_and_t[c + 1], t_banks[c + 1])
                 t3_and_t4[c + 1] = fourth_power(t2_f32[c + 1])
 
             if c + 2 < CHUNKS:
-                grouped[c + 2] = regroup_coef(loaded[c + 2][1], 1)
+                grouped[c + 2] = regroup_coef(coef_rows[c + 2])
             operands = {"ones": (ones_words, ones_scales, 0)}
             operands["x"], operands["t"] = quantise(
                 x_and_t[c][:].rearrange("p a g f -> p (a g f)"), ("x", "t")
             )
             multiply(c, operands, coef[c], (("x", None), ("ones", 0), ("t", 1)))
             if c + 2 < CHUNKS:
-                x_banks[c + 2] = turn_x(loaded[c + 2][0])
+                x_banks[c + 2] = turn_x(x_rows[c + 2])
                 coef[c + 2] = quantise_coef(grouped[c + 2])
             operands["t2"] = quantise(t2[:], ("t2",))[0]
             operands["t3"], operands["t4"] = quantise(

@@ -27,6 +27,7 @@ CHUNKS = GROUPS // G_CHUNK
 ACT_COLS = G_CHUNK * ROWS * PACK
 COEF_COLS = G_CHUNK * POWERS * OUTPUTS * PACK
 WIDEST_QUANTISE = 4096
+W_GROUPS = 4
 SPLIT = 3
 
 FLOPS = 2 * ROWS * FEATURES * OUTPUTS * (POWERS + 1)
@@ -41,6 +42,7 @@ def tile_kolmogorovarnoldlinear_k_kernel(
     coef_by_chunk = basis_coeffs.rearrange(
         "(c g p j) o n -> c p g (j o n)", g=G_CHUNK, p=P, j=PACK
     )
+    coef_by_output = basis_coeffs.rearrange("(g p j) o n -> g p j o n", p=P, j=PACK)
 
     with ExitStack() as ctx:
         const = ctx.enter_context(tc.tile_pool(name="const", bufs=1))
@@ -55,19 +57,41 @@ def tile_kolmogorovarnoldlinear_k_kernel(
         ctx.enter_context(tc.manual_schedule())
 
 
-        def load_x(c):
+        def new_x_rows():
             x_rows = loads.tile([P, G_CHUNK, HALVES, K_PASS], BF16)
-            for g in range(G_CHUNK):
-                nc.sync.dma_start(out=x_rows[:, g, :, :], in_=x_by_group[c * G_CHUNK + g])
             return x_rows
 
-        def load_coef(c, pieces):
+        def load_x_group(x_rows, c, g):
+            nc.sync.dma_start(out=x_rows[:, g, :, :], in_=x_by_group[c * G_CHUNK + g])
+
+        def load_x(c):
+            x_rows = new_x_rows()
+            for g in range(G_CHUNK):
+                load_x_group(x_rows, c, g)
+            return x_rows
+
+        def new_coef_rows():
             coef_rows = loads.tile([P, G_CHUNK, PACK * OUTPUTS * POWERS], BF16)
-            width = G_CHUNK // pieces
-            for i in range(pieces):
-                groups = slice(i * width, (i + 1) * width)
-                nc.sync.dma_start(out=coef_rows[:, groups, :], in_=coef_by_chunk[c][:, groups, :])
             return coef_rows
+
+        def load_coef(c):
+            coef_rows = new_coef_rows()
+            nc.sync.dma_start(out=coef_rows[:], in_=coef_by_chunk[c])
+            return coef_rows
+
+        def load_coef_outputs(coef_rows, c, g, outputs):
+            nc.sync.dma_start(
+                out=coef_rows[:, g, :].rearrange("p (j o n) -> p j o n", j=PACK, o=OUTPUTS)[:, :, outputs, :]
+                .rearrange("p j o n -> p j (o n)"),
+                in_=coef_by_output[c * G_CHUNK + g][:, :, outputs, :].rearrange("p j o n -> p j (o n)"),
+            )
+
+        def load_w(i):
+            groups = slice(i * W_GROUPS, (i + 1) * W_GROUPS)
+            nc.sync.dma_start(
+                out=w_words[:, groups, :].bitcast(I32),
+                in_=linear_w_words[groups].rearrange("g p o j -> p g (o j)").bitcast(I32),
+            )
 
         def tanh_rows(x_rows, pieces):
             t_rows = work.tile([P, G_CHUNK, HALVES, K_PASS], F32)
@@ -145,19 +169,20 @@ def tile_kolmogorovarnoldlinear_k_kernel(
             nc.vector.quantize_mx(out=words[:].bitcast(FP8X4), scales=scales[:], in_=values)
             return [(words, scales, i * ACT_COLS // PACK) for i in range(len(names))]
 
-        def regroup_coef(coef_rows):
+        def new_coef_grouped():
             coef_grouped = work.tile([P, G_CHUNK, POWERS, OUTPUTS, PACK], BF16, align_bytes=64)
+            return coef_grouped
+
+        def regroup_coef(coef_grouped, coef_rows, g, outputs):
             by_output_in = coef_rows[:].rearrange(
                 "p g (a b o n) -> p g o a n b", a=PACK // 2, b=2, o=OUTPUTS, n=POWERS
             )
             by_output_out = coef_grouped[:].rearrange("p g n o (a b) -> p g o a n b", b=2)
-            for g in range(G_CHUNK):
-                for powers in (slice(0, SPLIT), slice(SPLIT, POWERS)):
-                    nc.vector.tensor_copy(
-                        out=by_output_out[:, g, :, :, powers, :],
-                        in_=by_output_in[:, g, :, :, powers, :],
-                    )
-            return coef_grouped
+            for powers in (slice(0, SPLIT), slice(SPLIT, POWERS)):
+                nc.vector.tensor_copy(
+                    out=by_output_out[:, g, outputs, :, powers, :],
+                    in_=by_output_in[:, g, outputs, :, powers, :],
+                )
 
         def quantise_coef(coef_grouped):
             coef_words = coef_mx.tile([P, COEF_COLS // PACK], U32, align_bytes=64)
@@ -223,10 +248,18 @@ def tile_kolmogorovarnoldlinear_k_kernel(
         linear_sum = sums.tile([OUTPUTS, ROWS], F32)
 
 
-        x_rows = {0: load_x(0)}
-        coef_rows = {0: load_coef(0, G_CHUNK), 1: load_coef(1, 1)}
+        all_outputs = slice(0, OUTPUTS)
+        halves_of_outputs = (slice(0, OUTPUTS // 2), slice(OUTPUTS // 2, OUTPUTS))
+        x_rows = {0: new_x_rows()}
+        coef_rows = {0: new_coef_rows()}
+        load_x_group(x_rows[0], 0, 0)
+        load_coef_outputs(coef_rows[0], 0, 0, halves_of_outputs[0])
+        load_x_group(x_rows[0], 0, 1)
+        load_coef_outputs(coef_rows[0], 0, 0, halves_of_outputs[1])
+        load_coef_outputs(coef_rows[0], 0, 1, all_outputs)
+        coef_rows[1] = load_coef(1)
         x_rows[1] = load_x(1)
-        coef_rows[2] = load_coef(2, 1)
+        coef_rows[2] = load_coef(2)
         x_rows[2] = load_x(2)
         nc.sync.dma_start(out=balance_bf16[:], in_=pathway_balance.partition_broadcast(P))
         for quadrant in range(4):
@@ -236,20 +269,21 @@ def tile_kolmogorovarnoldlinear_k_kernel(
                 .rearrange("g q o -> q g o")
                 .bitcast(I32),
             )
-        nc.sync.dma_start(
-            out=w_words[:].bitcast(I32),
-            in_=linear_w_words.rearrange("g p o j -> p g (o j)").bitcast(I32),
-        )
+        load_w(0)
 
-        grouped = {}
         coef = {}
         t_rows = {0: tanh_rows(x_rows[0], G_CHUNK)}
         t_banks = {0: turn_t(t_rows[0])}
         x_banks = {0: turn_x(x_rows[0])}
-        grouped[0] = regroup_coef(coef_rows[0])
+        grouped = {0: new_coef_grouped()}
+        for outputs in halves_of_outputs:
+            regroup_coef(grouped[0], coef_rows[0], 0, outputs)
+        regroup_coef(grouped[0], coef_rows[0], 1, all_outputs)
         x_and_t = {0: work.tile([P, 2, G_CHUNK, ROWS * PACK], BF16, name="x_and_t", align_bytes=64)}
         coef[0] = quantise_coef(grouped[0])
-        grouped[1] = regroup_coef(coef_rows[1])
+        grouped[1] = new_coef_grouped()
+        for g in range(G_CHUNK):
+            regroup_coef(grouped[1], coef_rows[1], g, all_outputs)
         t2_f32 = {0: square(t_banks[0])}
         round_t(x_and_t[0], t_banks[0])
         x_out(x_and_t[0], x_banks[0])
@@ -263,8 +297,10 @@ def tile_kolmogorovarnoldlinear_k_kernel(
 
         for c in range(CHUNKS):
             if c + 3 < CHUNKS:
-                coef_rows[c + 3] = load_coef(c + 3, 1)
                 x_rows[c + 3] = load_x(c + 3)
+                coef_rows[c + 3] = load_coef(c + 3)
+            if (c + 1) * W_GROUPS < GROUPS:
+                load_w(c + 1)
 
             t2 = squares.tile([P, ACT_COLS], BF16, align_bytes=64)
             nc.gpsimd.tensor_scalar(
@@ -297,7 +333,9 @@ def tile_kolmogorovarnoldlinear_k_kernel(
                 t3_and_t4[c + 1] = fourth_power(t2_f32[c + 1])
 
             if c + 2 < CHUNKS:
-                grouped[c + 2] = regroup_coef(coef_rows[c + 2])
+                grouped[c + 2] = new_coef_grouped()
+                for g in range(G_CHUNK):
+                    regroup_coef(grouped[c + 2], coef_rows[c + 2], g, all_outputs)
             operands = {"ones": (ones_words, ones_scales, 0)}
             operands["x"], operands["t"] = quantise(
                 x_and_t[c][:].rearrange("p a g f -> p (a g f)"), ("x", "t")

@@ -26,7 +26,6 @@ K_CHUNK = G_CHUNK * K_PASS
 CHUNKS = GROUPS // G_CHUNK
 ACT_COLS = G_CHUNK * ROWS * PACK
 COEF_COLS = G_CHUNK * POWERS * OUTPUTS * PACK
-WIDEST_QUANTISE = 4096
 W_GROUPS = 4
 SPLIT = 3
 
@@ -157,45 +156,59 @@ def tile_kolmogorovarnoldlinear_k_kernel(
             for i, bank in enumerate(banks):
                 nc.scalar.copy(out=piece(t_bf16, i), in_=by_word(bank))
 
-        def fourth_power(t2_f32):
+        def fourth_power(t2_f32, pieces):
             t3_and_t4 = work.tile([P, 2, ACT_COLS], BF16, align_bytes=64)
-            nc.scalar.activation(out=t3_and_t4[:, 1, :], in_=t2_f32[:], func=ACT.Square)
+            width = ACT_COLS // pieces
+            for i in range(pieces):
+                columns = slice(i * width, (i + 1) * width)
+                nc.scalar.activation(out=t3_and_t4[:, 1, columns], in_=t2_f32[:, columns], func=ACT.Square)
             return t3_and_t4
 
-        def quantise(values, names):
+        def quantise(values, names, pieces=1):
             columns = len(names) * ACT_COLS // PACK
             words = act_mx.tile([P, columns], U32, name=names[0] + "_words", align_bytes=64)
             scales = act_mx.tile([P, columns], U8, name=names[0] + "_scales", align_bytes=64)
-            nc.vector.quantize_mx(out=words[:].bitcast(FP8X4), scales=scales[:], in_=values)
+            width = columns // pieces
+            for i in range(pieces):
+                part = slice(i * width, (i + 1) * width)
+                nc.vector.quantize_mx(
+                    out=words[:, part].bitcast(FP8X4),
+                    scales=scales[:, part],
+                    in_=values[:, i * width * PACK : (i + 1) * width * PACK],
+                )
             return [(words, scales, i * ACT_COLS // PACK) for i in range(len(names))]
 
         def new_coef_grouped():
             coef_grouped = work.tile([P, G_CHUNK, POWERS, OUTPUTS, PACK], BF16, align_bytes=64)
             return coef_grouped
 
-        def regroup_coef(coef_grouped, coef_rows, g, outputs):
+        def regroup_coef(copies, coef_grouped, coef_rows, g, outputs):
             by_output_in = coef_rows[:].rearrange(
                 "p g (a b o n) -> p g o a n b", a=PACK // 2, b=2, o=OUTPUTS, n=POWERS
             )
             by_output_out = coef_grouped[:].rearrange("p g n o (a b) -> p g o a n b", b=2)
-            for powers in (slice(0, SPLIT), slice(SPLIT, POWERS)):
-                nc.vector.tensor_copy(
+            for copy, powers in zip(copies, (slice(0, SPLIT), slice(SPLIT, POWERS))):
+                copy(
                     out=by_output_out[:, g, outputs, :, powers, :],
                     in_=by_output_in[:, g, outputs, :, powers, :],
                 )
 
-        def quantise_coef(coef_grouped):
+        def new_coef_mx():
             coef_words = coef_mx.tile([P, COEF_COLS // PACK], U32, align_bytes=64)
             coef_scales = coef_mx.tile([P, COEF_COLS // PACK], U8, align_bytes=64)
+            return coef_words, coef_scales
+
+        def quantise_coef(words_and_scales, coef_grouped, widths, first=0):
+            coef_words, coef_scales = words_and_scales
             values = coef_grouped[:].rearrange("p g n o j -> p (g n o j)")
-            for first in range(0, COEF_COLS, WIDEST_QUANTISE):
-                last = min(first + WIDEST_QUANTISE, COEF_COLS)
+            for width in widths:
+                last = first + width
                 nc.vector.quantize_mx(
                     out=coef_words[:, first // PACK : last // PACK].bitcast(FP8X4),
                     scales=coef_scales[:, first // PACK : last // PACK],
                     in_=values[:, first:last],
                 )
-            return coef_words, coef_scales
+                first = last
 
         def multiply(c, operands, coef, factors):
             coef_words, coef_scales = coef
@@ -248,6 +261,8 @@ def tile_kolmogorovarnoldlinear_k_kernel(
         linear_sum = sums.tile([OUTPUTS, ROWS], F32)
 
 
+        by_vector = (nc.vector.tensor_copy, nc.vector.tensor_copy)
+        by_both = (nc.vector.tensor_copy, nc.scalar.copy)
         all_outputs = slice(0, OUTPUTS)
         halves_of_outputs = (slice(0, OUTPUTS // 2), slice(OUTPUTS // 2, OUTPUTS))
         x_rows = {0: new_x_rows()}
@@ -271,26 +286,29 @@ def tile_kolmogorovarnoldlinear_k_kernel(
             )
         load_w(0)
 
-        coef = {}
+        group_widths = (2048, 512)
+        chunk_widths = (4096, 1024)
+        coef = {0: new_coef_mx(), 1: new_coef_mx()}
         t_rows = {0: tanh_rows(x_rows[0], G_CHUNK)}
         t_banks = {0: turn_t(t_rows[0])}
         x_banks = {0: turn_x(x_rows[0])}
         grouped = {0: new_coef_grouped()}
         for outputs in halves_of_outputs:
-            regroup_coef(grouped[0], coef_rows[0], 0, outputs)
-        regroup_coef(grouped[0], coef_rows[0], 1, all_outputs)
+            regroup_coef(by_vector, grouped[0], coef_rows[0], 0, outputs)
+        quantise_coef(coef[0], grouped[0], group_widths)
+        regroup_coef(by_vector, grouped[0], coef_rows[0], 1, all_outputs)
         x_and_t = {0: work.tile([P, 2, G_CHUNK, ROWS * PACK], BF16, name="x_and_t", align_bytes=64)}
-        coef[0] = quantise_coef(grouped[0])
+        quantise_coef(coef[0], grouped[0], group_widths, COEF_COLS // G_CHUNK)
         grouped[1] = new_coef_grouped()
         for g in range(G_CHUNK):
-            regroup_coef(grouped[1], coef_rows[1], g, all_outputs)
+            regroup_coef(by_vector, grouped[1], coef_rows[1], g, all_outputs)
         t2_f32 = {0: square(t_banks[0])}
         round_t(x_and_t[0], t_banks[0])
         x_out(x_and_t[0], x_banks[0])
         t_rows[1] = tanh_rows(x_rows[1], 1)
         x_banks[1] = turn_x(x_rows[1])
-        t3_and_t4 = {0: fourth_power(t2_f32[0])}
-        coef[1] = quantise_coef(grouped[1])
+        t3_and_t4 = {0: fourth_power(t2_f32[0], 1)}
+        quantise_coef(coef[1], grouped[1], chunk_widths)
 
         nc.gpsimd.tensor_copy(out=balance[:], in_=balance_bf16[:])
 
@@ -330,41 +348,64 @@ def tile_kolmogorovarnoldlinear_k_kernel(
                 x_out(x_and_t[c + 1], x_banks[c + 1])
                 t2_f32[c + 1] = square(t_banks[c + 1])
                 round_t(x_and_t[c + 1], t_banks[c + 1])
-                t3_and_t4[c + 1] = fourth_power(t2_f32[c + 1])
+                t3_and_t4[c + 1] = fourth_power(t2_f32[c + 1], 1 if c + 2 < CHUNKS else G_CHUNK)
 
             if c + 2 < CHUNKS:
                 grouped[c + 2] = new_coef_grouped()
                 for g in range(G_CHUNK):
-                    regroup_coef(grouped[c + 2], coef_rows[c + 2], g, all_outputs)
+                    regroup_coef(
+                        by_vector if c + 3 < CHUNKS or g == 0 else by_both,
+                        grouped[c + 2],
+                        coef_rows[c + 2],
+                        g,
+                        all_outputs,
+                    )
             operands = {"ones": (ones_words, ones_scales, 0)}
-            operands["x"], operands["t"] = quantise(
-                x_and_t[c][:].rearrange("p a g f -> p (a g f)"), ("x", "t")
-            )
-            multiply(c, operands, coef[c], (("x", None), ("ones", 0), ("t", 1)))
+            if c + 1 < CHUNKS:
+                operands["x"], operands["t"] = quantise(
+                    x_and_t[c][:].rearrange("p a g f -> p (a g f)"), ("x", "t")
+                )
+                multiply(c, operands, coef[c], (("x", None), ("ones", 0), ("t", 1)))
             if c + 2 < CHUNKS:
                 x_banks[c + 2] = turn_x(x_rows[c + 2])
-                coef[c + 2] = quantise_coef(grouped[c + 2])
+                coef[c + 2] = new_coef_mx()
+                if c + 3 < CHUNKS:
+                    quantise_coef(coef[c + 2], grouped[c + 2], chunk_widths)
+            elif c + 2 == CHUNKS:
+                quantise_coef(coef[c + 1], grouped[c + 1], chunk_widths)
+                last_x = quantise(x_and_t[c + 1][:, 0, :, :].rearrange("p g f -> p (g f)"), ("x",))
+                multiply(c + 1, {"x": last_x[0]}, coef[c + 1], (("x", None),))
             operands["t2"] = quantise(t2[:], ("t2",))[0]
-            operands["t3"], operands["t4"] = quantise(
-                t3_and_t4[c][:].rearrange("p a f -> p (a f)"), ("t3", "t4")
-            )
-            multiply(c, operands, coef[c], (("t2", 2), ("t3", 3), ("t4", 4)))
+            if c + 1 < CHUNKS:
+                operands["t3"], operands["t4"] = quantise(
+                    t3_and_t4[c][:].rearrange("p a f -> p (a f)"), ("t3", "t4")
+                )
+                multiply(c, operands, coef[c], (("t2", 2), ("t3", 3), ("t4", 4)))
+            else:
+                multiply(c, operands, coef[c], (("ones", 0), ("t2", 2)))
+                operands["t3"] = quantise(t3_and_t4[c][:, 0, :], ("t3",))[0]
+                multiply(c, operands, coef[c], (("t3", 3),))
+                operands["t"] = quantise(x_and_t[c][:, 1, :, :].rearrange("p g f -> p (g f)"), ("t",))[0]
+                multiply(c, operands, coef[c], (("t", 1),))
+                operands["t4"] = quantise(t3_and_t4[c][:, 1, :], ("t4",), G_CHUNK)[0]
+                multiply(c, operands, coef[c], (("t4", 4),))
 
 
         linear_part = const.tile([OUTPUTS, ROWS], F32)
         y_turned = const.tile([OUTPUTS, ROWS], F32)
         y = const.tile([P, HALVES, OUTPUTS], F32)
         nc.scalar.activation(out=linear_part[:], in_=linear_sum[:], func=ACT.Copy, scale=balance[:, 1:2])
-        nc.vector.scalar_tensor_tensor(
-            out=y_turned[:],
-            in0=basis_sum[:],
-            scalar=balance[:, 0:1],
-            in1=linear_part[:],
-            op0=ALU.mult,
-            op1=ALU.add,
-        )
         for h in range(HALVES):
+            rows = slice(h * P, (h + 1) * P)
+            nc.vector.scalar_tensor_tensor(
+                out=y_turned[:, rows],
+                in0=basis_sum[:, rows],
+                scalar=balance[:, 0:1],
+                in1=linear_part[:, rows],
+                op0=ALU.mult,
+                op1=ALU.add,
+            )
             y_bank = turned_x.tile([P, 2, ROWS], F32, name="bank")
-            nc.tensor.transpose(y_bank[:, 0, 0:OUTPUTS], y_turned[:, h * P : (h + 1) * P], identity[:])
-            nc.vector.tensor_copy(out=y[:, h, :], in_=y_bank[:, 0, 0:OUTPUTS])
+            nc.tensor.transpose(y_bank[:, 0, 0:OUTPUTS], y_turned[:, rows], identity[:])
+            nc.scalar.copy(out=y[:, h, :], in_=y_bank[:, 0, 0:OUTPUTS])
             nc.sync.dma_start(out=out[h], in_=y[:, h, :])

@@ -27,7 +27,8 @@ CHUNKS = GROUPS // G_CHUNK
 ACT_COLS = G_CHUNK * ROWS * PACK
 COEF_COLS = G_CHUNK * POWERS * OUTPUTS * PACK
 W_GROUPS = 4
-SPLIT = 3
+EARLY, LATE = slice(0, 3), slice(3, POWERS)
+SHARED_CHUNKS = (CHUNKS // 2, CHUNKS - 1)
 
 FLOPS = 2 * ROWS * FEATURES * OUTPUTS * (POWERS + 1)
 
@@ -182,12 +183,12 @@ def tile_kolmogorovarnoldlinear_k_kernel(
             coef_grouped = work.tile([P, G_CHUNK, POWERS, OUTPUTS, PACK], BF16, align_bytes=64)
             return coef_grouped
 
-        def regroup_coef(copies, coef_grouped, coef_rows, g, outputs):
+        def regroup_coef(copy, coef_grouped, coef_rows, g, outputs, parts=(EARLY, LATE)):
             by_output_in = coef_rows[:].rearrange(
                 "p g (a b o n) -> p g o a n b", a=PACK // 2, b=2, o=OUTPUTS, n=POWERS
             )
             by_output_out = coef_grouped[:].rearrange("p g n o (a b) -> p g o a n b", b=2)
-            for copy, powers in zip(copies, (slice(0, SPLIT), slice(SPLIT, POWERS))):
+            for powers in parts:
                 copy(
                     out=by_output_out[:, g, outputs, :, powers, :],
                     in_=by_output_in[:, g, outputs, :, powers, :],
@@ -261,8 +262,6 @@ def tile_kolmogorovarnoldlinear_k_kernel(
         linear_sum = sums.tile([OUTPUTS, ROWS], F32)
 
 
-        by_vector = (nc.vector.tensor_copy, nc.vector.tensor_copy)
-        by_both = (nc.vector.tensor_copy, nc.scalar.copy)
         all_outputs = slice(0, OUTPUTS)
         halves_of_outputs = (slice(0, OUTPUTS // 2), slice(OUTPUTS // 2, OUTPUTS))
         x_rows = {0: new_x_rows()}
@@ -294,14 +293,14 @@ def tile_kolmogorovarnoldlinear_k_kernel(
         x_banks = {0: turn_x(x_rows[0])}
         grouped = {0: new_coef_grouped()}
         for outputs in halves_of_outputs:
-            regroup_coef(by_vector, grouped[0], coef_rows[0], 0, outputs)
+            regroup_coef(nc.vector.tensor_copy, grouped[0], coef_rows[0], 0, outputs)
         quantise_coef(coef[0], grouped[0], group_widths)
-        regroup_coef(by_vector, grouped[0], coef_rows[0], 1, all_outputs)
+        regroup_coef(nc.vector.tensor_copy, grouped[0], coef_rows[0], 1, all_outputs)
         x_and_t = {0: work.tile([P, 2, G_CHUNK, ROWS * PACK], BF16, name="x_and_t", align_bytes=64)}
         quantise_coef(coef[0], grouped[0], group_widths, COEF_COLS // G_CHUNK)
         grouped[1] = new_coef_grouped()
         for g in range(G_CHUNK):
-            regroup_coef(by_vector, grouped[1], coef_rows[1], g, all_outputs)
+            regroup_coef(nc.vector.tensor_copy, grouped[1], coef_rows[1], g, all_outputs)
         t2_f32 = {0: square(t_banks[0])}
         round_t(x_and_t[0], t_banks[0])
         x_out(x_and_t[0], x_banks[0])
@@ -341,6 +340,9 @@ def tile_kolmogorovarnoldlinear_k_kernel(
 
             if c + 2 < CHUNKS:
                 t_rows[c + 2] = tanh_rows(x_rows[c + 2], 1)
+                grouped[c + 2] = new_coef_grouped()
+                if c + 2 in SHARED_CHUNKS:
+                    regroup_coef(nc.scalar.copy, grouped[c + 2], coef_rows[c + 2], 1, all_outputs, (LATE,))
             if c + 1 < CHUNKS:
                 x_and_t[c + 1] = work.tile(
                     [P, 2, G_CHUNK, ROWS * PACK], BF16, name="x_and_t", align_bytes=64
@@ -351,14 +353,10 @@ def tile_kolmogorovarnoldlinear_k_kernel(
                 t3_and_t4[c + 1] = fourth_power(t2_f32[c + 1], 1 if c + 2 < CHUNKS else G_CHUNK)
 
             if c + 2 < CHUNKS:
-                grouped[c + 2] = new_coef_grouped()
                 for g in range(G_CHUNK):
+                    parts = (EARLY,) if g == 1 and c + 2 in SHARED_CHUNKS else (EARLY, LATE)
                     regroup_coef(
-                        by_vector if c + 3 < CHUNKS or g == 0 else by_both,
-                        grouped[c + 2],
-                        coef_rows[c + 2],
-                        g,
-                        all_outputs,
+                        nc.vector.tensor_copy, grouped[c + 2], coef_rows[c + 2], g, all_outputs, parts
                     )
             operands = {"ones": (ones_words, ones_scales, 0)}
             if c + 1 < CHUNKS:

from contextlib import ExitStack

import concourse.mybir as mybir
from concourse.masks import make_identity

F32 = mybir.dt.float32
BF16 = mybir.dt.bfloat16
U32 = mybir.dt.uint32
U8 = mybir.dt.uint8
I32 = mybir.dt.int32
FP8X4 = mybir.dt.float8_e4m3fn_x4
ACT = mybir.ActivationFunctionType
ALU = mybir.AluOpType

P = 128
PACK = 4
K_PASS = P * PACK
HALVES = 2
ROWS = HALVES * P
FEATURES = 16384
OUTPUTS = 128
POWERS = 5
GROUPS = FEATURES // K_PASS
G_CHUNK = 2
K_CHUNK = G_CHUNK * K_PASS
CHUNKS = GROUPS // G_CHUNK
ACT_COLS = G_CHUNK * ROWS * PACK
COEF_COLS = G_CHUNK * POWERS * OUTPUTS * PACK
W_GROUPS = 4
EARLY, LATE = slice(0, 3), slice(3, POWERS)
SHARED_CHUNKS = (CHUNKS // 2, CHUNKS - 1)

FLOPS = 2 * ROWS * FEATURES * OUTPUTS * (POWERS + 1)


def tile_kolmogorovarnoldlinear_k_kernel(
    tc, x, basis_coeffs, linear_w_words, linear_w_scales, pathway_balance, out
):
    nc = tc.nc

    x_by_group = x.rearrange("h r (g k) -> g r h k", k=K_PASS)
    coef_by_chunk = basis_coeffs.rearrange(
        "(c g p j) o n -> c p g (j o n)", g=G_CHUNK, p=P, j=PACK
    )
    coef_by_output = basis_coeffs.rearrange("(g p j) o n -> g p j o n", p=P, j=PACK)

    with ExitStack() as ctx:
        const = ctx.enter_context(tc.tile_pool(name="const", bufs=1))
        loads = ctx.enter_context(tc.tile_pool(name="loads", bufs=3))
        work = ctx.enter_context(tc.tile_pool(name="work", bufs=2))
        squares = ctx.enter_context(tc.tile_pool(name="squares", bufs=1))
        act_mx = ctx.enter_context(tc.tile_pool(name="act_mx", bufs=2))
        coef_mx = ctx.enter_context(tc.tile_pool(name="coef_mx", bufs=3))
        sums = ctx.enter_context(tc.psum_pool(name="sums", bufs=1))
        turned_x = ctx.enter_context(tc.psum_pool(name="turned_x", bufs=G_CHUNK))
        turned_t = ctx.enter_context(tc.psum_pool(name="turned_t", bufs=G_CHUNK * HALVES))
        ctx.enter_context(tc.manual_schedule())


        def new_x_rows():
            x_rows = loads.tile([P, G_CHUNK, HALVES, K_PASS], BF16)
            return x_rows

        def load_x_group(x_rows, c, g):
            nc.sync.dma_start(out=x_rows[:, g, :, :], in_=x_by_group[c * G_CHUNK + g])

        def load_x(c):
            x_rows = new_x_rows()
            for g in range(G_CHUNK):
                load_x_group(x_rows, c, g)
            return x_rows

        def new_coef_rows():
            coef_rows = loads.tile([P, G_CHUNK, PACK * OUTPUTS * POWERS], BF16)
            return coef_rows

        def load_coef(c):
            coef_rows = new_coef_rows()
            nc.sync.dma_start(out=coef_rows[:], in_=coef_by_chunk[c])
            return coef_rows

        def load_coef_outputs(coef_rows, c, g, outputs):
            nc.sync.dma_start(
                out=coef_rows[:, g, :].rearrange("p (j o n) -> p j o n", j=PACK, o=OUTPUTS)[:, :, outputs, :]
                .rearrange("p j o n -> p j (o n)"),
                in_=coef_by_output[c * G_CHUNK + g][:, :, outputs, :].rearrange("p j o n -> p j (o n)"),
            )

        def load_w(i):
            groups = slice(i * W_GROUPS, (i + 1) * W_GROUPS)
            nc.sync.dma_start(
                out=w_words[:, groups, :].bitcast(I32),
                in_=linear_w_words[groups].rearrange("g p o j -> p g (o j)").bitcast(I32),
            )

        def tanh_rows(x_rows, pieces):
            t_rows = work.tile([P, G_CHUNK, HALVES, K_PASS], F32)
            width = G_CHUNK // pieces
            for i in range(pieces):
                groups = slice(i * width, (i + 1) * width)
                nc.scalar.activation(
                    out=t_rows[:, groups, :, :].rearrange("p g h k -> p (g h k)"),
                    in_=x_rows[:, groups, :, :].rearrange("p g h k -> p (g h k)"),
                    func=ACT.Tanh,
                )
            return t_rows

        def turn_x(x_rows):
            x_words = x_rows[:].rearrange("p g h k -> p (g h k)").bitcast(F32)
            banks = []
            for g in range(G_CHUNK):
                bank = turned_x.tile([P, 2, ROWS], F32)
                for u in range(2):
                    for h in range(HALVES):
                        first = (g * HALVES + h) * 2 * P
                        nc.tensor.transpose(
                            bank[:, u, h * P : (h + 1) * P],
                            x_words[:, first + u : first + 2 * P : 2],
                            identity[:],
                        )
                banks.append(bank)
            return banks

        def turn_t(t_rows):
            banks = []
            for g in range(G_CHUNK):
                for h in range(HALVES):
                    t_bank = turned_t.tile([P, PACK, P], F32)
                    for j in range(PACK):
                        nc.tensor.transpose(
                            t_bank[:, j, :], t_rows[:, g, h, j : K_PASS : PACK], identity[:]
                        )
                    banks.append(t_bank)
            return banks

        def x_out(x_and_t, banks):
            for g in range(G_CHUNK):
                nc.scalar.copy(
                    out=x_and_t[:, 0, g, :].bitcast(F32).rearrange("p (r u) -> p r u", u=2),
                    in_=banks[g][:].rearrange("p u r -> p r u"),
                )

        def by_word(bank):
            return bank[:].rearrange("p j r -> p r j")

        def piece(tile, i):
            return tile[:, i * P * PACK : (i + 1) * P * PACK].rearrange("p (r j) -> p r j", j=PACK)

        def square(banks):
            t2_f32 = work.tile([P, ACT_COLS], F32)
            for i, bank in enumerate(banks):
                nc.scalar.activation(out=piece(t2_f32, i), in_=by_word(bank), func=ACT.Square)
            return t2_f32

        def round_t(x_and_t, banks):
            t_bf16 = x_and_t[:, 1, :, :].rearrange("p g f -> p (g f)")
            for i, bank in enumerate(banks):
                nc.scalar.copy(out=piece(t_bf16, i), in_=by_word(bank))

        def fourth_power(t2_f32, pieces):
            t3_and_t4 = work.tile([P, 2, ACT_COLS], BF16, align_bytes=64)
            width = ACT_COLS // pieces
            for i in range(pieces):
                columns = slice(i * width, (i + 1) * width)
                nc.scalar.activation(out=t3_and_t4[:, 1, columns], in_=t2_f32[:, columns], func=ACT.Square)
            return t3_and_t4

        def quantise(values, names, pieces=1):
            columns = len(names) * ACT_COLS // PACK
            words = act_mx.tile([P, columns], U32, name=names[0] + "_words", align_bytes=64)
            scales = act_mx.tile([P, columns], U8, name=names[0] + "_scales", align_bytes=64)
            width = columns // pieces
            for i in range(pieces):
                part = slice(i * width, (i + 1) * width)
                nc.vector.quantize_mx(
                    out=words[:, part].bitcast(FP8X4),
                    scales=scales[:, part],
                    in_=values[:, i * width * PACK : (i + 1) * width * PACK],
                )
            return [(words, scales, i * ACT_COLS // PACK) for i in range(len(names))]

        def new_coef_grouped():
            coef_grouped = work.tile([P, G_CHUNK, POWERS, OUTPUTS, PACK], BF16, align_bytes=64)
            return coef_grouped

        def regroup_coef(copy, coef_grouped, coef_rows, g, outputs, parts=(EARLY, LATE)):
            by_output_in = coef_rows[:].rearrange(
                "p g (a b o n) -> p g o a n b", a=PACK // 2, b=2, o=OUTPUTS, n=POWERS
            )
            by_output_out = coef_grouped[:].rearrange("p g n o (a b) -> p g o a n b", b=2)
            for powers in parts:
                copy(
                    out=by_output_out[:, g, outputs, :, powers, :],
                    in_=by_output_in[:, g, outputs, :, powers, :],
                )

        def new_coef_mx():
            coef_words = coef_mx.tile([P, COEF_COLS // PACK], U32, align_bytes=64)
            coef_scales = coef_mx.tile([P, COEF_COLS // PACK], U8, align_bytes=64)
            return coef_words, coef_scales

        def quantise_coef(words_and_scales, coef_grouped, widths, first=0):
            coef_words, coef_scales = words_and_scales
            values = coef_grouped[:].rearrange("p g n o j -> p (g n o j)")
            for width in widths:
                last = first + width
                nc.vector.quantize_mx(
                    out=coef_words[:, first // PACK : last // PACK].bitcast(FP8X4),
                    scales=coef_scales[:, first // PACK : last // PACK],
                    in_=values[:, first:last],
                )
                first = last

        def multiply(c, operands, coef, factors):
            coef_words, coef_scales = coef
            for name, n in factors:
                words, scales, first_column = operands[name]
                for g in range(G_CHUNK):
                    group = c * G_CHUNK + g
                    first_row = first_column if name == "ones" else first_column + g * ROWS
                    rows = slice(first_row, first_row + ROWS)
                    if name == "x":
                        weights = w_words[:, group, :]
                        weight_scales = w_scales[:, group, :]
                        total = linear_sum
                    else:
                        outputs = slice((g * POWERS + n) * OUTPUTS, (g * POWERS + n + 1) * OUTPUTS)
                        weights = coef_words[:, outputs]
                        weight_scales = coef_scales[:, outputs]
                        total = basis_sum
                    nc.tensor.matmul_mx(
                        out=total[:],
                        lhsT=weights.bitcast(FP8X4),
                        lhsT_scale=weight_scales,
                        rhs=words[:, rows].bitcast(FP8X4),
                        rhs_scale=scales[:, rows],
                        start=(group == 0 and name in ("x", "ones")),
                        stop=(group == GROUPS - 1 and name in ("x", "t4")),
                    )


        warm = const.tile([P, 1], F32)
        nc.vector.memset(warm[:], 0.0)
        nc.scalar.activation(out=warm[:], in_=warm[:], func=ACT.Tanh)

        identity = const.tile([P, P], F32)
        make_identity(nc, identity[:])

        ones = const.tile([P, ROWS * PACK], BF16, align_bytes=64)
        nc.vector.memset(ones[:], 1.0)
        ones_words = const.tile([P, ROWS], U32, align_bytes=64)
        ones_scales = const.tile([P, ROWS], U8, align_bytes=64)
        nc.vector.quantize_mx(out=ones_words[:].bitcast(FP8X4), scales=ones_scales[:], in_=ones[:])

        w_scales = const.tile([P, GROUPS, OUTPUTS], U8, align_bytes=64)
        nc.vector.memset(w_scales[:].rearrange("p g o -> p (g o)").bitcast(I32), 0)
        w_words = const.tile([P, GROUPS, OUTPUTS], U32, align_bytes=64)
        balance_bf16 = const.tile([P, 2], BF16)
        balance = const.tile([P, 2], F32)

        basis_sum = sums.tile([OUTPUTS, ROWS], F32)
        linear_sum = sums.tile([OUTPUTS, ROWS], F32)


        all_outputs = slice(0, OUTPUTS)
        halves_of_outputs = (slice(0, OUTPUTS // 2), slice(OUTPUTS // 2, OUTPUTS))
        x_rows = {0: new_x_rows()}
        coef_rows = {0: new_coef_rows()}
        load_x_group(x_rows[0], 0, 0)
        load_coef_outputs(coef_rows[0], 0, 0, halves_of_outputs[0])
        load_x_group(x_rows[0], 0, 1)
        load_coef_outputs(coef_rows[0], 0, 0, halves_of_outputs[1])
        load_coef_outputs(coef_rows[0], 0, 1, all_outputs)
        coef_rows[1] = load_coef(1)
        x_rows[1] = load_x(1)
        coef_rows[2] = load_coef(2)
        x_rows[2] = load_x(2)
        nc.sync.dma_start(out=balance_bf16[:], in_=pathway_balance.partition_broadcast(P))
        for quadrant in range(4):
            nc.sync.dma_start(
                out=w_scales[32 * quadrant : 32 * quadrant + 4, :, :].bitcast(I32),
                in_=linear_w_scales[:, 4 * quadrant : 4 * quadrant + 4, :]
                .rearrange("g q o -> q g o")
                .bitcast(I32),
            )
        load_w(0)

        group_widths = (2048, 512)
        chunk_widths = (4096, 1024)
        coef = {0: new_coef_mx(), 1: new_coef_mx()}
        t_rows = {0: tanh_rows(x_rows[0], G_CHUNK)}
        t_banks = {0: turn_t(t_rows[0])}
        x_banks = {0: turn_x(x_rows[0])}
        grouped = {0: new_coef_grouped()}
        for outputs in halves_of_outputs:
            regroup_coef(nc.vector.tensor_copy, grouped[0], coef_rows[0], 0, outputs)
        quantise_coef(coef[0], grouped[0], group_widths)
        regroup_coef(nc.vector.tensor_copy, grouped[0], coef_rows[0], 1, all_outputs)
        x_and_t = {0: work.tile([P, 2, G_CHUNK, ROWS * PACK], BF16, name="x_and_t", align_bytes=64)}
        quantise_coef(coef[0], grouped[0], group_widths, COEF_COLS // G_CHUNK)
        grouped[1] = new_coef_grouped()
        for g in range(G_CHUNK):
            regroup_coef(nc.vector.tensor_copy, grouped[1], coef_rows[1], g, all_outputs)
        t2_f32 = {0: square(t_banks[0])}
        round_t(x_and_t[0], t_banks[0])
        x_out(x_and_t[0], x_banks[0])
        t_rows[1] = tanh_rows(x_rows[1], 1)
        x_banks[1] = turn_x(x_rows[1])
        t3_and_t4 = {0: fourth_power(t2_f32[0], 1)}
        quantise_coef(coef[1], grouped[1], chunk_widths)

        nc.gpsimd.tensor_copy(out=balance[:], in_=balance_bf16[:])


        for c in range(CHUNKS):
            if c + 3 < CHUNKS:
                x_rows[c + 3] = load_x(c + 3)
                coef_rows[c + 3] = load_coef(c + 3)
            if (c + 1) * W_GROUPS < GROUPS:
                load_w(c + 1)

            t2 = squares.tile([P, ACT_COLS], BF16, align_bytes=64)
            nc.gpsimd.tensor_scalar(
                out=t2[:],
                in0=t2_f32[c][:],
                scalar1=1.0,
                scalar2=0.0,
                op0=ALU.mult,
                op1=ALU.add,
            )
            for i, bank in enumerate(t_banks[c]):
                nc.vector.tensor_tensor(
                    out=piece(t3_and_t4[c][:, 0, :], i),
                    in0=piece(t2_f32[c], i),
                    in1=by_word(bank),
                    op=ALU.mult,
                )
            if c + 1 < CHUNKS:
                t_banks[c + 1] = turn_t(t_rows[c + 1])

            if c + 2 < CHUNKS:
                t_rows[c + 2] = tanh_rows(x_rows[c + 2], 1)
                grouped[c + 2] = new_coef_grouped()
                if c + 2 in SHARED_CHUNKS:
                    regroup_coef(nc.scalar.copy, grouped[c + 2], coef_rows[c + 2], 1, all_outputs, (LATE,))
            if c + 1 < CHUNKS:
                x_and_t[c + 1] = work.tile(
                    [P, 2, G_CHUNK, ROWS * PACK], BF16, name="x_and_t", align_bytes=64
                )
                x_out(x_and_t[c + 1], x_banks[c + 1])
                t2_f32[c + 1] = square(t_banks[c + 1])
                round_t(x_and_t[c + 1], t_banks[c + 1])
                t3_and_t4[c + 1] = fourth_power(t2_f32[c + 1], 1 if c + 2 < CHUNKS else G_CHUNK)

            if c + 2 < CHUNKS:
                for g in range(G_CHUNK):
                    parts = (EARLY,) if g == 1 and c + 2 in SHARED_CHUNKS else (EARLY, LATE)
                    regroup_coef(
                        nc.vector.tensor_copy, grouped[c + 2], coef_rows[c + 2], g, all_outputs, parts
                    )
            operands = {"ones": (ones_words, ones_scales, 0)}
            if c + 1 < CHUNKS:
                operands["x"], operands["t"] = quantise(
                    x_and_t[c][:].rearrange("p a g f -> p (a g f)"), ("x", "t")
                )
                multiply(c, operands, coef[c], (("x", None), ("ones", 0), ("t", 1)))
            if c + 2 < CHUNKS:
                x_banks[c + 2] = turn_x(x_rows[c + 2])
                coef[c + 2] = new_coef_mx()
                if c + 3 < CHUNKS:
                    quantise_coef(coef[c + 2], grouped[c + 2], chunk_widths)
            elif c + 2 == CHUNKS:
                quantise_coef(coef[c + 1], grouped[c + 1], chunk_widths)
                last_x = quantise(x_and_t[c + 1][:, 0, :, :].rearrange("p g f -> p (g f)"), ("x",))
                multiply(c + 1, {"x": last_x[0]}, coef[c + 1], (("x", None),))
            operands["t2"] = quantise(t2[:], ("t2",))[0]
            if c + 1 < CHUNKS:
                operands["t3"], operands["t4"] = quantise(
                    t3_and_t4[c][:].rearrange("p a f -> p (a f)"), ("t3", "t4")
                )
                multiply(c, operands, coef[c], (("t2", 2), ("t3", 3), ("t4", 4)))
            else:
                multiply(c, operands, coef[c], (("ones", 0), ("t2", 2)))
                operands["t3"] = quantise(t3_and_t4[c][:, 0, :], ("t3",))[0]
                multiply(c, operands, coef[c], (("t3", 3),))
                operands["t"] = quantise(x_and_t[c][:, 1, :, :].rearrange("p g f -> p (g f)"), ("t",))[0]
                multiply(c, operands, coef[c], (("t", 1),))
                operands["t4"] = quantise(t3_and_t4[c][:, 1, :], ("t4",), G_CHUNK)[0]
                multiply(c, operands, coef[c], (("t4", 4),))


        linear_part = const.tile([OUTPUTS, ROWS], F32)
        y_turned = const.tile([OUTPUTS, ROWS], F32)
        y = const.tile([P, HALVES, OUTPUTS], F32)
        nc.scalar.activation(out=linear_part[:], in_=linear_sum[:], func=ACT.Copy, scale=balance[:, 1:2])
        for h in range(HALVES):
            rows = slice(h * P, (h + 1) * P)
            nc.vector.scalar_tensor_tensor(
                out=y_turned[:, rows],
                in0=basis_sum[:, rows],
                scalar=balance[:, 0:1],
                in1=linear_part[:, rows],
                op0=ALU.mult,
                op1=ALU.add,
            )
            y_bank = turned_x.tile([P, 2, ROWS], F32, name="bank")
            nc.tensor.transpose(y_bank[:, 0, 0:OUTPUTS], y_turned[:, rows], identity[:])
            nc.scalar.copy(out=y[:, h, :], in_=y_bank[:, 0, 0:OUTPUTS])
            nc.sync.dma_start(out=out[h], in_=y[:, h, :])
